import numpy as np
import ml_dtypes


def mxq(x, axis, fmt="e4m3"):
    dtype, down = {"e4m3": (ml_dtypes.float8_e4m3fn, 7), "e5m2": (ml_dtypes.float8_e5m2, 14)}[fmt]
    v = np.moveaxis(np.asarray(x, np.float32).astype(ml_dtypes.bfloat16).astype(np.float64), axis, -1)
    blocks = v.reshape(v.shape[:-1] + (-1, 32))
    amax = np.abs(blocks).max(-1, keepdims=True)
    byte = np.maximum(np.where(amax > 0, np.frexp(amax)[1] - 1 + 127, 0) - down, 1)
    scale = np.exp2(byte - 127.0)
    codes = (blocks / scale).astype(np.float32).astype(dtype).astype(np.float64)
    return np.moveaxis((codes * scale).reshape(v.shape), -1, axis)


WIDE = False


def mx_kscale(k):
    if not WIDE:
        return np.ones(k)
    levels = np.array([10, -10, 5, -5, 0])
    a = np.random.permutation(np.resize(levels, k // 512 * 4)).reshape(k // 512, 4)
    idx = np.arange(k)
    return np.exp2(a[idx // 512, idx % 128 // 32])


BF16 = ml_dtypes.bfloat16


def bf(x):
    return np.asarray(x, np.float32).astype(BF16)


def f64(x):
    return np.asarray(x).astype(np.float64)


B, M, D, N = 2, 512, 512, 1024
NORM_EPS = 1e-12
SIG = 2.0


def silu(v):
    return v / (1.0 + np.exp(-v))


def l2norm(x, axis):
    n = np.sqrt(np.sum(x * x, axis=axis, keepdims=True))
    return x / np.maximum(n, NORM_EPS)


def setup_inputs():
    s = mx_kscale(D)
    return {"points": bf(np.random.standard_normal((B, D, N))),
            "clusters": bf(np.random.standard_normal((B, M, D)) * s),
            "sim_alpha": bf(SIG * np.sqrt(D) * (1.0 + 0.1 * np.random.standard_normal(M))),
            "sim_beta": bf(0.5 * np.random.standard_normal(M)),
            "clusters_bias": bf(0.3 * np.random.standard_normal((M, D)) * s),
            "Wc": bf(np.random.standard_normal((D, D)) / np.sqrt(D) / s[None, :]),
            "bc": bf(0.3 * np.random.standard_normal(D))}


def reference(points, clusters, sim_alpha, sim_beta, clusters_bias, Wc, bc):
    z = (mxq(f64(clusters) + f64(clusters_bias), 2, "e4m3") @ mxq(f64(Wc), 1, "e4m3").T) + f64(bc)
    cn = l2norm(silu(z), -1)
    pn = l2norm(f64(points), -2)
    sim = mxq(cn, 2, "e4m3") @ mxq(pn, 1, "e4m3")
    sim = f64(sim_alpha)[None, :, None] * sim + f64(sim_beta)[None, :, None]
    e = np.exp(sim - sim.max(axis=1, keepdims=True))
    return e / e.sum(axis=1, keepdims=True)

@@ -1,0 +1,292 @@
+from contextlib import ExitStack
+
+import concourse.mybir as mybir
+from concourse.masks import make_identity
+
+F32 = mybir.dt.float32
+BF16 = mybir.dt.bfloat16
+U32 = mybir.dt.uint32
+U8 = mybir.dt.uint8
+FP8X4 = mybir.dt.float8_e4m3fn_x4
+ACT = mybir.ActivationFunctionType
+ALU = mybir.AluOpType
+AX = mybir.AxisListType
+
+P = 128
+B, M, D, N = 2, 512, 512, 1024
+FLOPS = 2 * B * M * D * D + 2 * B * M * D * N
+EPS2 = 1e-24
+
+
+def tile_fuzzyclustering_pa_kernel(
+    tc, points, clusters, sim_alpha, sim_beta, clusters_bias, Wc, bc, out
+):
+    nc = tc.nc
+    with ExitStack() as ctx:
+        keep = ctx.enter_context(tc.tile_pool(name="keep", bufs=1))
+        work = ctx.enter_context(tc.tile_pool(name="work", bufs=2))
+        psum = ctx.enter_context(tc.psum_pool(name="psum", bufs=2))
+
+        def bank(tag, bufs, name, dtype=F32, width=512):
+            return psum.tile([P, width], dtype, tag=tag, bufs=bufs, name=name)
+
+        ident_f = keep.tile([P, P], F32, name="ident_f")
+        make_identity(nc, ident_f[:])
+        ident_b = keep.tile([P, P], BF16, name="ident_b")
+        make_identity(nc, ident_b[:])
+        mhalf = keep.tile([P, 8], F32, name="mhalf")
+        nc.vector.memset(mhalf[:], -0.5)
+        small = keep.tile([P, P], BF16, name="small")
+        nc.vector.memset(small[:], 0.0)
+        warm = keep.tile([P, 1], F32, name="warm")
+        nc.vector.memset(warm[:], 0.0)
+        warm2 = keep.tile([P, 1], F32, name="warm2")
+        nc.scalar.activation(out=warm2[:], in_=warm[:], func=ACT.Silu)
+
+        bias_sb = keep.tile([P, 4, D], BF16, name="bias_sb")
+        cl_sb = keep.tile([P, 8, D], BF16, name="cl_sb")
+        wc_sb = keep.tile([P, 4, D], BF16, name="wc_sb")
+        pts = keep.tile([P, B, 4, N], BF16, name="pts")
+        nc.sync.dma_start(out=small[0:4, :], in_=sim_alpha.rearrange("(t p) -> t p", p=P))
+        nc.sync.dma_start(out=small[4:8, :], in_=sim_beta.rearrange("(t p) -> t p", p=P))
+        nc.sync.dma_start(out=small[8:12, :], in_=bc.rearrange("(t p) -> t p", p=P))
+        nc.sync.dma_start(out=bias_sb[:], in_=clusters_bias.rearrange("(g p) k -> p g k", p=P))
+        nc.sync.dma_start(out=cl_sb[:, 0:4, :], in_=clusters[0].rearrange("(g p) k -> p g k", p=P))
+        nc.sync.dma_start(out=wc_sb[:], in_=Wc.rearrange("(g p) k -> p g k", p=P))
+        nc.sync.dma_start(out=cl_sb[:, 4:8, :], in_=clusters[1].rearrange("(g p) k -> p g k", p=P))
+        for b in range(B):
+            nc.sync.dma_start(out=pts[:, b, :, :], in_=points[b].rearrange("(t p) n -> p t n", p=P))
+
+        gbias = keep.tile([P, M, 4], BF16, name="gbias", align_bytes=64)
+        gw = keep.tile([P, D, 4], BF16, name="gw", align_bytes=64)
+        gx = keep.tile([P, B * M, 4], BF16, name="gx", align_bytes=64)
+        wq = keep.tile([P, D], U32, name="wq", align_bytes=64)
+        ws = keep.tile([P, D], U8, name="ws", align_bytes=64)
+        xq = keep.tile([P, B * M], U32, name="xq", align_bytes=64)
+        xs = keep.tile([P, B * M], U8, name="xs", align_bytes=64)
+
+        def word_transposes(src, g0):
+            t = bank("fw", 3, "wt")
+            srcw = src[:].bitcast(F32)
+            for g2 in range(2):
+                for u in range(2):
+                    c0 = 256 * u + 128 * g2
+                    nc.tensor.transpose(
+                        t[:, c0 : c0 + 128], srcw[:, g0 + g2, 128 * u : 128 * u + 128], ident_f[:]
+                    )
+            return t
+
+        def words_out(dst, src, g0):
+            t = word_transposes(src, g0)
+            nc.scalar.copy(
+                out=dst[:].bitcast(F32)[:, 128 * g0 : 128 * g0 + 256, :],
+                in_=t[:].rearrange("q (u c) -> q c u", u=2),
+            )
+
+        def quantise(grouped, codes, scales, c0, cols):
+            nc.vector.quantize_mx(
+                out=codes[:, c0 : c0 + cols].bitcast(FP8X4),
+                scales=scales[:, c0 : c0 + cols],
+                in_=grouped[:, c0 : c0 + cols, :].rearrange("p c t -> p (c t)"),
+            )
+
+        def x_part(b):
+            for h in range(2):
+                g0 = 4 * b + 2 * h
+                t = word_transposes(cl_sb, g0)
+                nc.vector.tensor_tensor(
+                    out=gx[:, 128 * g0 : 128 * g0 + 256, :].rearrange("q c (u e) -> q c u e", u=2),
+                    in0=t[:].bitcast(BF16).rearrange("q (u c e) -> q c u e", u=2, e=2),
+                    in1=gbias[:, 256 * h : 256 * h + 256, :].rearrange("q c (u e) -> q c u e", u=2),
+                    op=ALU.add,
+                )
+            quantise(gx, xq, xs, M * b, M)
+
+        words_out(gbias, bias_sb, 0)
+        words_out(gbias, bias_sb, 2)
+        x_part(0)
+        cst_ps = bank("fw", 3, "cst_ps", BF16, P)
+        nc.tensor.transpose(cst_ps[:], small[:], ident_b[:])
+        cst = keep.tile([P, 12], F32, name="cst")
+        nc.vector.tensor_copy(out=cst[:], in_=cst_ps[:, 0:12])
+        words_out(gw, wc_sb, 0)
+        words_out(gw, wc_sb, 2)
+        quantise(gw, wq, ws, 0, D)
+        x_part(1)
+
+        c_sb = keep.tile([P, 4, B * M], F32, name="c_sb")
+        junk = keep.tile([P, 512], BF16, name="junk")
+        ss_c = keep.tile([P, 8], F32, name="ss_c")
+        cl_c = keep.tile([P, 8], F32, name="cl_c")
+        rn_c = keep.tile([P, 8], F32, name="rn_c")
+        gc = keep.tile([P, B * M, 4], BF16, name="gc", align_bytes=64)
+        cq = keep.tile([P, B * M], U32, name="cq", align_bytes=64)
+        cs = keep.tile([P, B * M], U8, name="cs", align_bytes=64)
+
+        def centres_a(b):
+            for ot in range(4):
+                z = bank("mx", 2, "z")
+                nc.tensor.matmul_mx(
+                    out=z[:],
+                    lhsT=wq[:, 128 * ot : 128 * ot + 128].bitcast(FP8X4),
+                    lhsT_scale=ws[:, 128 * ot : 128 * ot + 128],
+                    rhs=xq[:, M * b : M * b + M].bitcast(FP8X4),
+                    rhs_scale=xs[:, M * b : M * b + M],
+                    start=True,
+                    stop=True,
+                )
+                nc.scalar.activation(
+                    out=c_sb[:, ot, M * b : M * b + M],
+                    in_=z[:],
+                    func=ACT.Silu,
+                    bias=cst[:, 8 + ot : 9 + ot],
+                    scale=1.0,
+                )
+
+        def centres_b(b):
+            for mt in range(4):
+                g = 4 * b + mt
+                ct = bank("fw", 3, "ct")
+                for ot in range(4):
+                    nc.tensor.transpose(
+                        ct[:, 128 * ot : 128 * ot + 128],
+                        c_sb[:, ot, 128 * g : 128 * g + 128],
+                        ident_f[:],
+                    )
+                nc.scalar.activation(
+                    out=junk[:], in_=ct[:], func=ACT.Square, accum_out=ss_c[:, g : g + 1]
+                )
+            sl = slice(4 * b, 4 * b + 4)
+            nc.gpsimd.tensor_scalar(
+                out=cl_c[:, sl], in0=ss_c[:, sl], scalar1=EPS2, scalar2=None, op0=ALU.max
+            )
+            nc.gpsimd.tensor_tensor(out=rn_c[:, sl], in0=cl_c[:, sl], in1=mhalf[:, 0:4], op=ALU.pow)
+            rc = bank("bk", 3, "rc")
+            for mt in range(4):
+                g = 4 * b + mt
+                nc.tensor.transpose(
+                    rc[:, 128 * mt : 128 * mt + 128],
+                    rn_c[:, g : g + 1].to_broadcast([P, P]),
+                    ident_f[:],
+                )
+            nc.vector.tensor_tensor(
+                out=gc[:, M * b : M * b + M, :],
+                in0=rc[:].unsqueeze(2).to_broadcast([P, M, 4]),
+                in1=c_sb[:, :, M * b : M * b + M].rearrange("p t m -> p m t"),
+                op=ALU.mult,
+            )
+            quantise(gc, cq, cs, M * b, M)
+
+        ss_p = keep.tile([P, 16], F32, name="ss_p")
+        cl_p = keep.tile([P, 16], F32, name="cl_p")
+        rn_p = keep.tile([P, 16], F32, name="rn_p")
+        gp = keep.tile([P, B * N, 4], BF16, name="gp", align_bytes=64)
+        pq = keep.tile([P, B * N], U32, name="pq", align_bytes=64)
+        pscl = keep.tile([P, B * N], U8, name="pscl", align_bytes=64)
+        ptw = pts[:].bitcast(F32)
+
+        def points_block(b, j):
+            bj = 4 * b + j
+            f = bank("fw", 3, "f")
+            for t in range(4):
+                nc.tensor.transpose(
+                    f[:, 128 * t : 128 * t + 128], ptw[:, b, t, 128 * j : 128 * j + 128], ident_f[:]
+                )
+            fb = f[:].bitcast(BF16).rearrange("w (d e) -> w e d", e=2)
+            for e in range(2):
+                nc.scalar.activation(
+                    out=junk[:],
+                    in_=fb[:, e, :],
+                    func=ACT.Square,
+                    accum_out=ss_p[:, 2 * bj + e : 2 * bj + e + 1],
+                )
+            sl = slice(2 * bj, 2 * bj + 2)
+            nc.gpsimd.tensor_scalar(
+                out=cl_p[:, sl], in0=ss_p[:, sl], scalar1=EPS2, scalar2=None, op0=ALU.max
+            )
+            nc.gpsimd.tensor_tensor(out=rn_p[:, sl], in0=cl_p[:, sl], in1=mhalf[:, 0:2], op=ALU.pow)
+            rb = bank("bk", 3, "rb", F32, 256)
+            for e in range(2):
+                nc.tensor.transpose(
+                    rb[:, 128 * e : 128 * e + 128],
+                    rn_p[:, 2 * bj + e : 2 * bj + e + 1].to_broadcast([P, P]),
+                    ident_f[:],
+                )
+            n0 = 256 * j
+            nc.vector.tensor_tensor(
+                out=gp[:, N * b + n0 : N * b + n0 + 256, :].rearrange("p (w e) t -> p w e t", e=2),
+                in0=rb[:].rearrange("p (e w) -> p w e", e=2).unsqueeze(3).to_broadcast([P, P, 2, 4]),
+                in1=pts[:, b, :, n0 : n0 + 256].rearrange("p t (w e) -> p w e t", e=2),
+                op=ALU.mult,
+            )
+            if j % 2 == 1:
+                quantise(gp, pq, pscl, N * b + 256 * (j - 1), 512)
+
+        def tail_chunk(b, h):
+            lsb = work.tile([P, 4, 512], F32, name="lsb", tag="lsb", bufs=2)
+            for mt in range(4):
+                s = bank("mx", 2, "s")
+                c0 = M * b + 128 * mt
+                n0 = N * b + 512 * h
+                nc.tensor.matmul_mx(
+                    out=s[:],
+                    lhsT=cq[:, c0 : c0 + 128].bitcast(FP8X4),
+                    lhsT_scale=cs[:, c0 : c0 + 128],
+                    rhs=pq[:, n0 : n0 + 512].bitcast(FP8X4),
+                    rhs_scale=pscl[:, n0 : n0 + 512],
+                    start=True,
+                    stop=True,
+                )
+                nc.scalar.activation(
+                    out=lsb[:, mt, :],
+                    in_=s[:],
+                    func=ACT.Identity,
+                    bias=cst[:, 4 + mt : 5 + mt],
+                    scale=cst[:, mt : mt + 1],
+                )
+            ost = work.tile([P, 4, 512], F32, name="ost", tag="ost", bufs=2)
+            for i in range(4):
+                lt = bank("fw", 3, "lt")
+                for mt in range(4):
+                    nc.tensor.transpose(
+                        lt[:, 128 * mt : 128 * mt + 128],
+                        lsb[:, mt, 128 * i : 128 * i + 128],
+                        ident_f[:],
+                    )
+                nmx = work.tile([P, 1], F32, name="nmx", tag="nmx", bufs=4)
+                nc.vector.tensor_reduce(out=nmx[:], in_=lt[:], axis=AX.X, op=ALU.max, negate=True)
+                et = work.tile([P, 512], F32, name="et", tag="et", bufs=4)
+                sm = work.tile([P, 1], F32, name="sm", tag="sm", bufs=4)
+                nc.scalar.activation(
+                    out=et[:], in_=lt[:], func=ACT.Exp, bias=nmx[:], scale=1.0, accum_out=sm[:]
+                )
+                rs = work.tile([P, 1], F32, name="rs", tag="rs", bufs=4)
+                nc.vector.reciprocal(out=rs[:], in_=sm[:])
+                nc.gpsimd.tensor_scalar(
+                    out=et[:], in0=et[:], scalar1=rs[:], scalar2=0.0, op0=ALU.mult, op1=ALU.add
+                )
+                o = bank("bk", 3, "o")
+                for mt in range(4):
+                    nc.tensor.transpose(
+                        o[:, 128 * mt : 128 * mt + 128], et[:, 128 * mt : 128 * mt + 128], ident_f[:]
+                    )
+                nc.vector.tensor_copy(
+                    out=ost[:, :, 128 * i : 128 * i + 128],
+                    in_=o[:].rearrange("p (t n) -> p t n", t=4),
+                )
+            nc.sync.dma_start(
+                out=out[b].rearrange("(t p) n -> p t n", p=P)[:, :, 512 * h : 512 * h + 512],
+                in_=ost[:],
+            )
+
+        centres_a(0)
+        centres_a(1)
+        for j in range(4):
+            points_block(0, j)
+        centres_b(0)
+        centres_b(1)
+        for j in range(4):
+            points_block(1, j)
+        for b in range(B):
+            for h in range(2):
+                tail_chunk(b, h)

@@ -30,6 +30,8 @@ def tile_fuzzyclustering_pa_kernel(
         def bank(tag, bufs, name, dtype=F32, width=512):
             return psum.tile([P, width], dtype, tag=tag, bufs=bufs, name=name)
 
+        ctx.enter_context(tc.manual_schedule())
+
         ident_f = keep.tile([P, P], F32, name="ident_f")
         make_identity(nc, ident_f[:])
         ident_b = keep.tile([P, P], BF16, name="ident_b")
@@ -47,16 +49,26 @@ def tile_fuzzyclustering_pa_kernel(
         cl_sb = keep.tile([P, 8, D], BF16, name="cl_sb")
         wc_sb = keep.tile([P, 4, D], BF16, name="wc_sb")
         pts = keep.tile([P, B, 4, N], BF16, name="pts")
+
+        def load_points(b, h):
+            nc.sync.dma_start(
+                out=pts[:, b, :, 512 * h : 512 * h + 512],
+                in_=points[b].rearrange("(t p) n -> p t n", p=P)[:, :, 512 * h : 512 * h + 512],
+            )
+
         nc.sync.dma_start(out=small[0:4, :], in_=sim_alpha.rearrange("(t p) -> t p", p=P))
         nc.sync.dma_start(out=small[4:8, :], in_=sim_beta.rearrange("(t p) -> t p", p=P))
         nc.sync.dma_start(out=small[8:12, :], in_=bc.rearrange("(t p) -> t p", p=P))
         nc.sync.dma_start(out=bias_sb[:], in_=clusters_bias.rearrange("(g p) k -> p g k", p=P))
         nc.sync.dma_start(out=cl_sb[:, 0:4, :], in_=clusters[0].rearrange("(g p) k -> p g k", p=P))
         nc.sync.dma_start(out=wc_sb[:], in_=Wc.rearrange("(g p) k -> p g k", p=P))
+        load_points(0, 0)
         nc.sync.dma_start(out=cl_sb[:, 4:8, :], in_=clusters[1].rearrange("(g p) k -> p g k", p=P))
-        for b in range(B):
-            nc.sync.dma_start(out=pts[:, b, :, :], in_=points[b].rearrange("(t p) n -> p t n", p=P))
+        load_points(0, 1)
+        load_points(1, 0)
+        load_points(1, 1)
 
+        cst = keep.tile([P, 12], F32, name="cst")
         gbias = keep.tile([P, M, 4], BF16, name="gbias", align_bytes=64)
         gw = keep.tile([P, D, 4], BF16, name="gw", align_bytes=64)
         gx = keep.tile([P, B * M, 4], BF16, name="gx", align_bytes=64)
@@ -64,6 +76,29 @@ def tile_fuzzyclustering_pa_kernel(
         ws = keep.tile([P, D], U8, name="ws", align_bytes=64)
         xq = keep.tile([P, B * M], U32, name="xq", align_bytes=64)
         xs = keep.tile([P, B * M], U8, name="xs", align_bytes=64)
+        c_sb = keep.tile([P, 4, B * M], F32, name="c_sb")
+        junk = keep.tile([P, 512], BF16, name="junk")
+        ss_c = keep.tile([P, 8], F32, name="ss_c")
+        cl_c = keep.tile([P, 8], F32, name="cl_c")
+        rn_c = keep.tile([P, 8], F32, name="rn_c")
+        gc = keep.tile([P, B * M, 4], BF16, name="gc", align_bytes=64)
+        cq = keep.tile([P, B * M], U32, name="cq", align_bytes=64)
+        cs = keep.tile([P, B * M], U8, name="cs", align_bytes=64)
+        ss_p = keep.tile([P, 16], F32, name="ss_p")
+        cl_p = keep.tile([P, 16], F32, name="cl_p")
+        rn_p = keep.tile([P, 16], F32, name="rn_p")
+        gp = keep.tile([P, B * N, 4], BF16, name="gp", align_bytes=64)
+        pq = keep.tile([P, B * N], U32, name="pq", align_bytes=64)
+        pscl = keep.tile([P, B * N], U8, name="pscl", align_bytes=64)
+        ptw = pts[:].bitcast(F32)
+        live = {}
+
+        def quantise(grouped, codes, scales, c0, cols):
+            nc.vector.quantize_mx(
+                out=codes[:, c0 : c0 + cols].bitcast(FP8X4),
+                scales=scales[:, c0 : c0 + cols],
+                in_=grouped[:, c0 : c0 + cols, :].rearrange("p c t -> p (c t)"),
+            )
 
         def word_transposes(src, g0):
             t = bank("fw", 3, "wt")
@@ -83,47 +118,31 @@ def tile_fuzzyclustering_pa_kernel(
                 in_=t[:].rearrange("q (u c) -> q c u", u=2),
             )
 
-        def quantise(grouped, codes, scales, c0, cols):
-            nc.vector.quantize_mx(
-                out=codes[:, c0 : c0 + cols].bitcast(FP8X4),
-                scales=scales[:, c0 : c0 + cols],
-                in_=grouped[:, c0 : c0 + cols, :].rearrange("p c t -> p (c t)"),
-            )
+        def tok_b():
+            words_out(gbias, bias_sb, 0)
+            words_out(gbias, bias_sb, 2)
 
-        def x_part(b):
+        def tok_w():
+            words_out(gw, wc_sb, 0)
+            words_out(gw, wc_sb, 2)
+            quantise(gw, wq, ws, 0, D)
+            cst_ps = bank("fw", 3, "cst_ps", BF16, P)
+            nc.tensor.transpose(cst_ps[:], small[:], ident_b[:])
+            nc.vector.tensor_copy(out=cst[:], in_=cst_ps[:, 0:12])
+
+        def tok_x(b):
+            ts = [word_transposes(cl_sb, 4 * b + 2 * h) for h in range(2)]
             for h in range(2):
                 g0 = 4 * b + 2 * h
-                t = word_transposes(cl_sb, g0)
                 nc.vector.tensor_tensor(
                     out=gx[:, 128 * g0 : 128 * g0 + 256, :].rearrange("q c (u e) -> q c u e", u=2),
-                    in0=t[:].bitcast(BF16).rearrange("q (u c e) -> q c u e", u=2, e=2),
+                    in0=ts[h][:].bitcast(BF16).rearrange("q (u c e) -> q c u e", u=2, e=2),
                     in1=gbias[:, 256 * h : 256 * h + 256, :].rearrange("q c (u e) -> q c u e", u=2),
                     op=ALU.add,
                 )
             quantise(gx, xq, xs, M * b, M)
 
-        words_out(gbias, bias_sb, 0)
-        words_out(gbias, bias_sb, 2)
-        x_part(0)
-        cst_ps = bank("fw", 3, "cst_ps", BF16, P)
-        nc.tensor.transpose(cst_ps[:], small[:], ident_b[:])
-        cst = keep.tile([P, 12], F32, name="cst")
-        nc.vector.tensor_copy(out=cst[:], in_=cst_ps[:, 0:12])
-        words_out(gw, wc_sb, 0)
-        words_out(gw, wc_sb, 2)
-        quantise(gw, wq, ws, 0, D)
-        x_part(1)
-
-        c_sb = keep.tile([P, 4, B * M], F32, name="c_sb")
-        junk = keep.tile([P, 512], BF16, name="junk")
-        ss_c = keep.tile([P, 8], F32, name="ss_c")
-        cl_c = keep.tile([P, 8], F32, name="cl_c")
-        rn_c = keep.tile([P, 8], F32, name="rn_c")
-        gc = keep.tile([P, B * M, 4], BF16, name="gc", align_bytes=64)
-        cq = keep.tile([P, B * M], U32, name="cq", align_bytes=64)
-        cs = keep.tile([P, B * M], U8, name="cs", align_bytes=64)
-
-        def centres_a(b):
+        def tok_z(b):
             for ot in range(4):
                 z = bank("mx", 2, "z")
                 nc.tensor.matmul_mx(
@@ -143,7 +162,7 @@ def tile_fuzzyclustering_pa_kernel(
                     scale=1.0,
                 )
 
-        def centres_b(b):
+        def tok_c_pre(b):
             for mt in range(4):
                 g = 4 * b + mt
                 ct = bank("fw", 3, "ct")
@@ -161,6 +180,8 @@ def tile_fuzzyclustering_pa_kernel(
                 out=cl_c[:, sl], in0=ss_c[:, sl], scalar1=EPS2, scalar2=None, op0=ALU.max
             )
             nc.gpsimd.tensor_tensor(out=rn_c[:, sl], in0=cl_c[:, sl], in1=mhalf[:, 0:4], op=ALU.pow)
+
+        def tok_c_post(b):
             rc = bank("bk", 3, "rc")
             for mt in range(4):
                 g = 4 * b + mt
@@ -177,15 +198,7 @@ def tile_fuzzyclustering_pa_kernel(
             )
             quantise(gc, cq, cs, M * b, M)
 
-        ss_p = keep.tile([P, 16], F32, name="ss_p")
-        cl_p = keep.tile([P, 16], F32, name="cl_p")
-        rn_p = keep.tile([P, 16], F32, name="rn_p")
-        gp = keep.tile([P, B * N, 4], BF16, name="gp", align_bytes=64)
-        pq = keep.tile([P, B * N], U32, name="pq", align_bytes=64)
-        pscl = keep.tile([P, B * N], U8, name="pscl", align_bytes=64)
-        ptw = pts[:].bitcast(F32)
-
-        def points_block(b, j):
+        def tok_f_pre(b, j):
             bj = 4 * b + j
             f = bank("fw", 3, "f")
             for t in range(4):
@@ -205,6 +218,9 @@ def tile_fuzzyclustering_pa_kernel(
                 out=cl_p[:, sl], in0=ss_p[:, sl], scalar1=EPS2, scalar2=None, op0=ALU.max
             )
             nc.gpsimd.tensor_tensor(out=rn_p[:, sl], in0=cl_p[:, sl], in1=mhalf[:, 0:2], op=ALU.pow)
+
+        def tok_f_post(b, j):
+            bj = 4 * b + j
             rb = bank("bk", 3, "rb", F32, 256)
             for e in range(2):
                 nc.tensor.transpose(
@@ -222,71 +238,150 @@ def tile_fuzzyclustering_pa_kernel(
             if j % 2 == 1:
                 quantise(gp, pq, pscl, N * b + 256 * (j - 1), 512)
 
-        def tail_chunk(b, h):
-            lsb = work.tile([P, 4, 512], F32, name="lsb", tag="lsb", bufs=2)
-            for mt in range(4):
-                s = bank("mx", 2, "s")
-                c0 = M * b + 128 * mt
-                n0 = N * b + 512 * h
-                nc.tensor.matmul_mx(
-                    out=s[:],
-                    lhsT=cq[:, c0 : c0 + 128].bitcast(FP8X4),
-                    lhsT_scale=cs[:, c0 : c0 + 128],
-                    rhs=pq[:, n0 : n0 + 512].bitcast(FP8X4),
-                    rhs_scale=pscl[:, n0 : n0 + 512],
-                    start=True,
-                    stop=True,
-                )
-                nc.scalar.activation(
-                    out=lsb[:, mt, :],
-                    in_=s[:],
-                    func=ACT.Identity,
-                    bias=cst[:, 4 + mt : 5 + mt],
-                    scale=cst[:, mt : mt + 1],
-                )
-            ost = work.tile([P, 4, 512], F32, name="ost", tag="ost", bufs=2)
-            for i in range(4):
-                lt = bank("fw", 3, "lt")
-                for mt in range(4):
-                    nc.tensor.transpose(
-                        lt[:, 128 * mt : 128 * mt + 128],
-                        lsb[:, mt, 128 * i : 128 * i + 128],
-                        ident_f[:],
-                    )
-                nmx = work.tile([P, 1], F32, name="nmx", tag="nmx", bufs=4)
-                nc.vector.tensor_reduce(out=nmx[:], in_=lt[:], axis=AX.X, op=ALU.max, negate=True)
-                et = work.tile([P, 512], F32, name="et", tag="et", bufs=4)
-                sm = work.tile([P, 1], F32, name="sm", tag="sm", bufs=4)
-                nc.scalar.activation(
-                    out=et[:], in_=lt[:], func=ACT.Exp, bias=nmx[:], scale=1.0, accum_out=sm[:]
-                )
-                rs = work.tile([P, 1], F32, name="rs", tag="rs", bufs=4)
-                nc.vector.reciprocal(out=rs[:], in_=sm[:])
-                nc.gpsimd.tensor_scalar(
-                    out=et[:], in0=et[:], scalar1=rs[:], scalar2=0.0, op0=ALU.mult, op1=ALU.add
-                )
-                o = bank("bk", 3, "o")
-                for mt in range(4):
-                    nc.tensor.transpose(
-                        o[:, 128 * mt : 128 * mt + 128], et[:, 128 * mt : 128 * mt + 128], ident_f[:]
-                    )
-                nc.vector.tensor_copy(
-                    out=ost[:, :, 128 * i : 128 * i + 128],
-                    in_=o[:].rearrange("p (t n) -> p t n", t=4),
-                )
-            nc.sync.dma_start(
-                out=out[b].rearrange("(t p) n -> p t n", p=P)[:, :, 512 * h : 512 * h + 512],
-                in_=ost[:],
+        def sim_pass(c, mt):
+            b, h = divmod(c, 2)
+            s = bank("mx", 2, "s")
+            c0 = M * b + 128 * mt
+            n0 = N * b + 512 * h
+            nc.tensor.matmul_mx(
+                out=s[:],
+                lhsT=cq[:, c0 : c0 + 128].bitcast(FP8X4),
+                lhsT_scale=cs[:, c0 : c0 + 128],
+                rhs=pq[:, n0 : n0 + 512].bitcast(FP8X4),
+                rhs_scale=pscl[:, n0 : n0 + 512],
+                start=True,
+                stop=True,
+            )
+            live[("s", c, mt)] = s
+
+        def logits(c, mt):
+            if mt == 0:
+                live[("l", c)] = work.tile([P, 4, 512], F32, name="lsb", tag="lsb", bufs=2)
+            nc.scalar.activation(
+                out=live[("l", c)][:, mt, :],
+                in_=live[("s", c, mt)][:],
+                func=ACT.Identity,
+                bias=cst[:, 4 + mt : 5 + mt],
+                scale=cst[:, mt : mt + 1],
             )
 
-        centres_a(0)
-        centres_a(1)
-        for j in range(4):
-            points_block(0, j)
-        centres_b(0)
-        centres_b(1)
-        for j in range(4):
-            points_block(1, j)
-        for b in range(B):
-            for h in range(2):
-                tail_chunk(b, h)
+        def fwd(k):
+            c, i = divmod(k, 4)
+            lt = bank("fw", 3, "lt")
+            for mt in range(4):
+                nc.tensor.transpose(
+                    lt[:, 128 * mt : 128 * mt + 128],
+                    live[("l", c)][:, mt, 128 * i : 128 * i + 128],
+                    ident_f[:],
+                )
+            live[("lt", k)] = lt
+
+        def col_max(k):
+            nmx = work.tile([P, 1], F32, name="nmx", tag="nmx", bufs=6)
+            nc.vector.tensor_reduce(
+                out=nmx[:], in_=live[("lt", k)][:], axis=AX.X, op=ALU.max, negate=True
+            )
+            live[("nmx", k)] = nmx
+
+        def col_exp(k):
+            et = work.tile([P, 512], F32, name="et", tag="et", bufs=5)
+            sm = work.tile([P, 1], F32, name="sm", tag="sm", bufs=6)
+            nc.scalar.activation(
+                out=et[:],
+                in_=live[("lt", k)][:],
+                func=ACT.Exp,
+                bias=live[("nmx", k)][:],
+                scale=1.0,
+                accum_out=sm[:],
+            )
+            live[("et", k)] = et
+            live[("sm", k)] = sm
+
+        def col_scale(k):
+            rs = work.tile([P, 1], F32, name="rs", tag="rs", bufs=6)
+            nc.vector.reciprocal(out=rs[:], in_=live[("sm", k)][:])
+            et = live[("et", k)]
+            nc.gpsimd.tensor_scalar(
+                out=et[:], in0=et[:], scalar1=rs[:], scalar2=0.0, op0=ALU.mult, op1=ALU.add
+            )
+
+        def bwd(k):
+            o = bank("bk", 3, "o")
+            et = live[("et", k)]
+            for mt in range(4):
+                nc.tensor.transpose(
+                    o[:, 128 * mt : 128 * mt + 128], et[:, 128 * mt : 128 * mt + 128], ident_f[:]
+                )
+            live[("o", k)] = o
+
+        def evac(k):
+            c, i = divmod(k, 4)
+            if i == 0:
+                live[("ost", c)] = work.tile([P, 4, 512], F32, name="ost", tag="ost", bufs=2)
+            ost = live[("ost", c)]
+            nc.vector.tensor_copy(
+                out=ost[:, :, 128 * i : 128 * i + 128],
+                in_=live[("o", k)][:].rearrange("p (t n) -> p t n", t=4),
+            )
+            if i == 3:
+                b, h = divmod(c, 2)
+                nc.sync.dma_start(
+                    out=out[b].rearrange("(t p) n -> p t n", p=P)[:, :, 512 * h : 512 * h + 512],
+                    in_=ost[:],
+                )
+
+        tok_b()
+        tok_x(0)
+        tok_w()
+        tok_f_pre(0, 0)
+        tok_f_pre(0, 1)
+        tok_x(1)
+        tok_z(0)
+        tok_f_post(0, 0)
+        tok_f_post(0, 1)
+        tok_f_pre(0, 2)
+        tok_f_pre(0, 3)
+        tok_c_pre(0)
+        tok_f_post(0, 2)
+        tok_f_post(0, 3)
+        tok_z(1)
+        tok_c_post(0)
+        tok_f_pre(1, 0)
+        tok_f_pre(1, 1)
+        tok_c_pre(1)
+        tok_f_post(1, 0)
+        tok_f_post(1, 1)
+        tok_f_pre(1, 2)
+        tok_f_pre(1, 3)
+        tok_c_post(1)
+        tok_f_post(1, 2)
+        tok_f_post(1, 3)
+
+        for mt in range(4):
+            sim_pass(0, mt)
+            logits(0, mt)
+        units = 16
+        for p in range(-2, units + 3):
+            if 0 <= p + 1 < units:
+                fwd(p + 1)
+            if 0 <= p < units:
+                col_max(p)
+            if 0 <= p - 1 < units:
+                col_scale(p - 1)
+            for c in range(1, 4):
+                for mt in range(4):
+                    if p == 4 * (c - 1) + mt - 1:
+                        logits(c, mt)
+            for c in range(1, 4):
+                if p == 4 * (c - 1) - 2:
+                    sim_pass(c, 0)
+                    sim_pass(c, 1)
+                if p == 4 * (c - 1):
+                    sim_pass(c, 2)
+                    sim_pass(c, 3)
+            if 0 <= p < units:
+                col_exp(p)
+            if 0 <= p - 2 < units:
+                bwd(p - 2)
+            if 0 <= p - 3 < units:
+                evac(p - 3)

@@ -28,7 +28,7 @@ def tile_fuzzyclustering_pa_kernel(
         psum = ctx.enter_context(tc.psum_pool(name="psum", bufs=2))
 
         def bank(tag, bufs, name, dtype=F32, width=512):
-            return psum.tile([P, width], dtype, tag=tag, bufs=bufs, name=name)
+            return psum.tile([P, width], dtype, tag="ps", bufs=8, name=name)
 
         ctx.enter_context(tc.manual_schedule())
 
@@ -284,7 +284,7 @@ def tile_fuzzyclustering_pa_kernel(
             live[("nmx", k)] = nmx
 
         def col_exp(k):
-            et = work.tile([P, 512], F32, name="et", tag="et", bufs=5)
+            et = work.tile([P, 512], F32, name="et", tag="et", bufs=6)
             sm = work.tile([P, 1], F32, name="sm", tag="sm", bufs=6)
             nc.scalar.activation(
                 out=et[:],
@@ -361,9 +361,11 @@ def tile_fuzzyclustering_pa_kernel(
             sim_pass(0, mt)
             logits(0, mt)
         units = 16
-        for p in range(-2, units + 3):
+        for p in range(-2, units + 5):
             if 0 <= p + 1 < units:
                 fwd(p + 1)
+            if 0 <= p - 5 < units:
+                evac(p - 5)
             if 0 <= p < units:
                 col_max(p)
             if 0 <= p - 1 < units:
@@ -381,7 +383,5 @@ def tile_fuzzyclustering_pa_kernel(
                     sim_pass(c, 3)
             if 0 <= p < units:
                 col_exp(p)
-            if 0 <= p - 2 < units:
-                bwd(p - 2)
             if 0 <= p - 3 < units:
-                evac(p - 3)
+                bwd(p - 3)

@@ -28,7 +28,7 @@ def tile_fuzzyclustering_pa_kernel(
         psum = ctx.enter_context(tc.psum_pool(name="psum", bufs=2))
 
         def bank(tag, bufs, name, dtype=F32, width=512):
-            return psum.tile([P, width], dtype, tag="ps", bufs=8, name=name)
+            return psum.tile([P, width], dtype, tag="ps", bufs=7, name=name)
 
         ctx.enter_context(tc.manual_schedule())
 
@@ -357,8 +357,23 @@ def tile_fuzzyclustering_pa_kernel(
         tok_f_post(1, 2)
         tok_f_post(1, 3)
 
+        scratch = psum.tile([P, 512], F32, tag="dm", bufs=1, name="scratch")
+
+        def keep_clock(n):
+            for i in range(n):
+                nc.tensor.matmul_mx(
+                    out=scratch[:],
+                    lhsT=cq[:, 0:128].bitcast(FP8X4),
+                    lhsT_scale=cs[:, 0:128],
+                    rhs=pq[:, 0:512].bitcast(FP8X4),
+                    rhs_scale=pscl[:, 0:512],
+                    start=True,
+                    stop=True,
+                )
+
         for mt in range(4):
             sim_pass(0, mt)
+        for mt in range(4):
             logits(0, mt)
         units = 16
         for p in range(-2, units + 5):
@@ -374,13 +389,11 @@ def tile_fuzzyclustering_pa_kernel(
                 for mt in range(4):
                     if p == 4 * (c - 1) + mt - 1:
                         logits(c, mt)
-            for c in range(1, 4):
-                if p == 4 * (c - 1) - 2:
-                    sim_pass(c, 0)
-                    sim_pass(c, 1)
-                if p == 4 * (c - 1):
-                    sim_pass(c, 2)
-                    sim_pass(c, 3)
+            real = [(c, mt) for c in range(1, 4) for mt in range(4) if p == 4 * (c - 1) + mt - 2]
+            for c, mt in real:
+                sim_pass(c, mt)
+            if p < units + 3:
+                keep_clock(2 - len(real))
             if 0 <= p < units:
                 col_exp(p)
             if 0 <= p - 3 < units:

@@ -28,7 +28,7 @@ def tile_fuzzyclustering_pa_kernel(
         psum = ctx.enter_context(tc.psum_pool(name="psum", bufs=2))
 
         def bank(tag, bufs, name, dtype=F32, width=512):
-            return psum.tile([P, width], dtype, tag="ps", bufs=7, name=name)
+            return psum.tile([P, width], dtype, tag="ps", bufs=8, name=name)
 
         ctx.enter_context(tc.manual_schedule())
 
@@ -323,60 +323,22 @@ def tile_fuzzyclustering_pa_kernel(
                 out=ost[:, :, 128 * i : 128 * i + 128],
                 in_=live[("o", k)][:].rearrange("p (t n) -> p t n", t=4),
             )
-            if i == 3:
-                b, h = divmod(c, 2)
-                nc.sync.dma_start(
-                    out=out[b].rearrange("(t p) n -> p t n", p=P)[:, :, 512 * h : 512 * h + 512],
-                    in_=ost[:],
-                )
+            b, h = divmod(c, 2)
+            rows = out[b].rearrange("(t p) n -> p t n", p=P)
+            if c == 3:
+                n0 = 512 * h + 128 * i
+                nc.sync.dma_start(out=rows[:, :, n0 : n0 + 128], in_=ost[:, :, 128 * i : 128 * i + 128])
+            elif i == 3:
+                nc.sync.dma_start(out=rows[:, :, 512 * h : 512 * h + 512], in_=ost[:])
 
-        tok_b()
-        tok_x(0)
-        tok_w()
-        tok_f_pre(0, 0)
-        tok_f_pre(0, 1)
-        tok_x(1)
-        tok_z(0)
-        tok_f_post(0, 0)
-        tok_f_post(0, 1)
-        tok_f_pre(0, 2)
-        tok_f_pre(0, 3)
-        tok_c_pre(0)
-        tok_f_post(0, 2)
-        tok_f_post(0, 3)
-        tok_z(1)
-        tok_c_post(0)
-        tok_f_pre(1, 0)
-        tok_f_pre(1, 1)
-        tok_c_pre(1)
-        tok_f_post(1, 0)
-        tok_f_post(1, 1)
-        tok_f_pre(1, 2)
-        tok_f_pre(1, 3)
-        tok_c_post(1)
-        tok_f_post(1, 2)
-        tok_f_post(1, 3)
-
-        scratch = psum.tile([P, 512], F32, tag="dm", bufs=1, name="scratch")
-
-        def keep_clock(n):
-            for i in range(n):
-                nc.tensor.matmul_mx(
-                    out=scratch[:],
-                    lhsT=cq[:, 0:128].bitcast(FP8X4),
-                    lhsT_scale=cs[:, 0:128],
-                    rhs=pq[:, 0:512].bitcast(FP8X4),
-                    rhs_scale=pscl[:, 0:512],
-                    start=True,
-                    stop=True,
-                )
-
-        for mt in range(4):
-            sim_pass(0, mt)
-        for mt in range(4):
-            logits(0, mt)
         units = 16
-        for p in range(-2, units + 5):
+
+        def prologue():
+            for mt in range(4):
+                sim_pass(0, mt)
+                logits(0, mt)
+
+        def step(p):
             if 0 <= p + 1 < units:
                 fwd(p + 1)
             if 0 <= p - 5 < units:
@@ -389,12 +351,53 @@ def tile_fuzzyclustering_pa_kernel(
                 for mt in range(4):
                     if p == 4 * (c - 1) + mt - 1:
                         logits(c, mt)
-            real = [(c, mt) for c in range(1, 4) for mt in range(4) if p == 4 * (c - 1) + mt - 2]
-            for c, mt in real:
-                sim_pass(c, mt)
-            if p < units + 3:
-                keep_clock(2 - len(real))
+            for c in range(1, 4):
+                if p == 4 * (c - 1) - 2:
+                    sim_pass(c, 0)
+                    sim_pass(c, 1)
+                if p == 4 * (c - 1):
+                    sim_pass(c, 2)
+                    sim_pass(c, 3)
             if 0 <= p < units:
                 col_exp(p)
             if 0 <= p - 3 < units:
                 bwd(p - 3)
+
+        def keep_clock():
+            scratch = bank("ps", 8, "scratch")
+            for i in range(2):
+                nc.tensor.matmul_mx(
+                    out=scratch[:],
+                    lhsT=wq[:, 0:128].bitcast(FP8X4),
+                    lhsT_scale=ws[:, 0:128],
+                    rhs=wq[:, 0:512].bitcast(FP8X4),
+                    rhs_scale=ws[:, 0:512],
+                    start=True,
+                    stop=True,
+                )
+
+        todo = {
+            "D": (keep_clock,),
+            "B": (tok_b,),
+            "W": (tok_w,),
+            "P": (prologue,),
+        }
+        for b in range(B):
+            todo["X%d" % b] = (tok_x, b)
+            todo["Z%d" % b] = (tok_z, b)
+            todo["C%d" % b] = (tok_c_pre, b)
+            todo["c%d" % b] = (tok_c_post, b)
+            for j in range(4):
+                todo["F%d%d" % (b, j)] = (tok_f_pre, b, j)
+                todo["f%d%d" % (b, j)] = (tok_f_post, b, j)
+        order = [
+            "B", "X0", "W", "F00", "F01", "Z0", "F10", "f00", "X1", "F02", "f01", "C0", "F11", "f10", "Z1", "f02", "c0", "F03", "D", "C1", "f11", "F12", "f03", "P", "F13", "c1", "T", "T", "T", "f12", "T", "f13", "T", "D", "T", "D", "T", "T", "T", "T", "T", "T", "T", "T", "T", "T", "T", "D", "T", "T", "T", "T", "T", "T",
+        ]
+        p = -2
+        for name in order:
+            if name == "T":
+                step(p)
+                p += 1
+            else:
+                todo[name][0](*todo[name][1:])
+        assert p == units + 5

@@ -301,9 +301,7 @@ def tile_fuzzyclustering_pa_kernel(
             rs = work.tile([P, 1], F32, name="rs", tag="rs", bufs=6)
             nc.vector.reciprocal(out=rs[:], in_=live[("sm", k)][:])
             et = live[("et", k)]
-            nc.gpsimd.tensor_scalar(
-                out=et[:], in0=et[:], scalar1=rs[:], scalar2=0.0, op0=ALU.mult, op1=ALU.add
-            )
+            nc.vector.tensor_scalar(out=et[:], in0=et[:], scalar1=rs[:], scalar2=None, op0=ALU.mult)
 
         def bwd(k):
             o = bank("bk", 3, "o")
@@ -319,7 +317,8 @@ def tile_fuzzyclustering_pa_kernel(
             if i == 0:
                 live[("ost", c)] = work.tile([P, 4, 512], F32, name="ost", tag="ost", bufs=2)
             ost = live[("ost", c)]
-            nc.vector.tensor_copy(
+            copy_out = nc.scalar.copy if i == 0 else nc.vector.tensor_copy
+            copy_out(
                 out=ost[:, :, 128 * i : 128 * i + 128],
                 in_=live[("o", k)][:].rearrange("p (t n) -> p t n", t=4),
             )

@@ -13,9 +13,13 @@ ALU = mybir.AluOpType
 AX = mybir.AxisListType
 
 P = 128
+G = 4
 B, M, D, N = 2, 512, 512, 1024
+CHUNK = 512
+BLOCK = 256
+TILES = B * N // P
 FLOPS = 2 * B * M * D * D + 2 * B * M * D * N
-EPS2 = 1e-24
+NORM_EPS_SQUARED = 1e-24
 
 
 def tile_fuzzyclustering_pa_kernel(
@@ -25,378 +29,337 @@ def tile_fuzzyclustering_pa_kernel(
     with ExitStack() as ctx:
         keep = ctx.enter_context(tc.tile_pool(name="keep", bufs=1))
         work = ctx.enter_context(tc.tile_pool(name="work", bufs=2))
-        psum = ctx.enter_context(tc.psum_pool(name="psum", bufs=2))
-
-        def bank(tag, bufs, name, dtype=F32, width=512):
-            return psum.tile([P, width], dtype, tag="ps", bufs=8, name=name)
-
+        psum = ctx.enter_context(tc.psum_pool(name="psum", bufs=8))
         ctx.enter_context(tc.manual_schedule())
 
-        ident_f = keep.tile([P, P], F32, name="ident_f")
-        make_identity(nc, ident_f[:])
-        ident_b = keep.tile([P, P], BF16, name="ident_b")
-        make_identity(nc, ident_b[:])
-        mhalf = keep.tile([P, 8], F32, name="mhalf")
-        nc.vector.memset(mhalf[:], -0.5)
-        small = keep.tile([P, P], BF16, name="small")
-        nc.vector.memset(small[:], 0.0)
-        warm = keep.tile([P, 1], F32, name="warm")
-        nc.vector.memset(warm[:], 0.0)
-        warm2 = keep.tile([P, 1], F32, name="warm2")
-        nc.scalar.activation(out=warm2[:], in_=warm[:], func=ACT.Silu)
+        def bank(name, width=CHUNK):
+            return psum.tile([P, width], F32, tag="bank", name=name)
 
-        bias_sb = keep.tile([P, 4, D], BF16, name="bias_sb")
-        cl_sb = keep.tile([P, 8, D], BF16, name="cl_sb")
-        wc_sb = keep.tile([P, 4, D], BF16, name="wc_sb")
-        pts = keep.tile([P, B, 4, N], BF16, name="pts")
+        alpha_bf = keep.tile([P, G], BF16, name="alpha_bf")
+        beta_bf = keep.tile([P, G], BF16, name="beta_bf")
+        bc_bf = keep.tile([P, G], BF16, name="bc_bf")
+        bias_sb = keep.tile([P, G, D], BF16, name="bias_sb")
+        cl_sb = keep.tile([P, B * G, D], BF16, name="cl_sb")
+        wc_sb = keep.tile([P, G, D], BF16, name="wc_sb")
+        pts = keep.tile([P, B, G, N], BF16, name="pts")
+        nc.scalar.dma_start(out=bc_bf[:], in_=bc.rearrange("(p g) -> p g", g=G))
+        nc.scalar.dma_start(out=alpha_bf[:], in_=sim_alpha.rearrange("(p g) -> p g", g=G))
+        nc.scalar.dma_start(out=beta_bf[:], in_=sim_beta.rearrange("(p g) -> p g", g=G))
 
-        def load_points(b, h):
+        def load_clusters(b):
             nc.sync.dma_start(
-                out=pts[:, b, :, 512 * h : 512 * h + 512],
-                in_=points[b].rearrange("(t p) n -> p t n", p=P)[:, :, 512 * h : 512 * h + 512],
+                out=cl_sb[:, G * b : G * b + G, :], in_=clusters[b].rearrange("(p g) k -> p g k", g=G)
             )
 
-        nc.sync.dma_start(out=small[0:4, :], in_=sim_alpha.rearrange("(t p) -> t p", p=P))
-        nc.sync.dma_start(out=small[4:8, :], in_=sim_beta.rearrange("(t p) -> t p", p=P))
-        nc.sync.dma_start(out=small[8:12, :], in_=bc.rearrange("(t p) -> t p", p=P))
-        nc.sync.dma_start(out=bias_sb[:], in_=clusters_bias.rearrange("(g p) k -> p g k", p=P))
-        nc.sync.dma_start(out=cl_sb[:, 0:4, :], in_=clusters[0].rearrange("(g p) k -> p g k", p=P))
-        nc.sync.dma_start(out=wc_sb[:], in_=Wc.rearrange("(g p) k -> p g k", p=P))
+        def load_points(b, half):
+            cols = slice(CHUNK * half, CHUNK * half + CHUNK)
+            nc.sync.dma_start(
+                out=pts[:, b, :, cols], in_=points[b].rearrange("(p t) n -> p t n", t=G)[:, :, cols]
+            )
+
+        nc.sync.dma_start(out=bias_sb[:], in_=clusters_bias.rearrange("(p g) k -> p g k", g=G))
+        load_clusters(0)
+        nc.sync.dma_start(out=wc_sb[:], in_=Wc.rearrange("(p g) k -> p g k", g=G))
         load_points(0, 0)
-        nc.sync.dma_start(out=cl_sb[:, 4:8, :], in_=clusters[1].rearrange("(g p) k -> p g k", p=P))
+        load_clusters(1)
         load_points(0, 1)
         load_points(1, 0)
         load_points(1, 1)
 
-        cst = keep.tile([P, 12], F32, name="cst")
-        gbias = keep.tile([P, M, 4], BF16, name="gbias", align_bytes=64)
-        gw = keep.tile([P, D, 4], BF16, name="gw", align_bytes=64)
-        gx = keep.tile([P, B * M, 4], BF16, name="gx", align_bytes=64)
-        wq = keep.tile([P, D], U32, name="wq", align_bytes=64)
-        ws = keep.tile([P, D], U8, name="ws", align_bytes=64)
-        xq = keep.tile([P, B * M], U32, name="xq", align_bytes=64)
-        xs = keep.tile([P, B * M], U8, name="xs", align_bytes=64)
-        c_sb = keep.tile([P, 4, B * M], F32, name="c_sb")
-        junk = keep.tile([P, 512], BF16, name="junk")
-        ss_c = keep.tile([P, 8], F32, name="ss_c")
-        cl_c = keep.tile([P, 8], F32, name="cl_c")
-        rn_c = keep.tile([P, 8], F32, name="rn_c")
-        gc = keep.tile([P, B * M, 4], BF16, name="gc", align_bytes=64)
-        cq = keep.tile([P, B * M], U32, name="cq", align_bytes=64)
-        cs = keep.tile([P, B * M], U8, name="cs", align_bytes=64)
-        ss_p = keep.tile([P, 16], F32, name="ss_p")
-        cl_p = keep.tile([P, 16], F32, name="cl_p")
-        rn_p = keep.tile([P, 16], F32, name="rn_p")
-        gp = keep.tile([P, B * N, 4], BF16, name="gp", align_bytes=64)
-        pq = keep.tile([P, B * N], U32, name="pq", align_bytes=64)
-        pscl = keep.tile([P, B * N], U8, name="pscl", align_bytes=64)
-        ptw = pts[:].bitcast(F32)
+        identity = keep.tile([P, P], F32, name="identity")
+        make_identity(nc, identity[:])
+        minus_half = keep.tile([P, G], F32, name="minus_half")
+        nc.vector.memset(minus_half[:], -0.5)
+        zero = keep.tile([P, 1], F32, name="zero")
+        nc.vector.memset(zero[:], 0.0)
+        warm = keep.tile([P, 1], F32, name="warm")
+        nc.scalar.activation(out=warm[:], in_=zero[:], func=ACT.Silu)
+
+        alpha = keep.tile([P, G], F32, name="alpha")
+        beta = keep.tile([P, G], F32, name="beta")
+        bc_f = keep.tile([P, G], F32, name="bc_f")
+        bias_grouped = keep.tile([P, M, G], BF16, name="bias_grouped", align_bytes=64)
+        w_grouped = keep.tile([P, D, G], BF16, name="w_grouped", align_bytes=64)
+        x_grouped = keep.tile([P, B * M, G], BF16, name="x_grouped", align_bytes=64)
+        c_grouped = keep.tile([P, B * M, G], BF16, name="c_grouped", align_bytes=64)
+        p_grouped = keep.tile([P, B * N, G], BF16, name="p_grouped", align_bytes=64)
+        w_codes = keep.tile([P, D], U32, name="w_codes", align_bytes=64)
+        w_scales = keep.tile([P, D], U8, name="w_scales", align_bytes=64)
+        x_codes = keep.tile([P, B * M], U32, name="x_codes", align_bytes=64)
+        x_scales = keep.tile([P, B * M], U8, name="x_scales", align_bytes=64)
+        c_codes = keep.tile([P, B * M], U32, name="c_codes", align_bytes=64)
+        c_scales = keep.tile([P, B * M], U8, name="c_scales", align_bytes=64)
+        p_codes = keep.tile([P, B * N], U32, name="p_codes", align_bytes=64)
+        p_scales = keep.tile([P, B * N], U8, name="p_scales", align_bytes=64)
+        c_sb = keep.tile([P, G, B * M], F32, name="c_sb")
+        squares = keep.tile([P, CHUNK], BF16, name="squares")
+        c_sumsq = keep.tile([P, B * G], F32, name="c_sumsq")
+        c_clamped = keep.tile([P, B * G], F32, name="c_clamped")
+        c_rnorm = keep.tile([P, B * G], F32, name="c_rnorm")
+        p_sumsq = keep.tile([P, 2 * B * G], F32, name="p_sumsq")
+        p_clamped = keep.tile([P, 2 * B * G], F32, name="p_clamped")
+        p_rnorm = keep.tile([P, 2 * B * G], F32, name="p_rnorm")
+        pts_words = pts[:].bitcast(F32)
         live = {}
 
-        def quantise(grouped, codes, scales, c0, cols):
+        def quantise(grouped, codes, scales, first, cols):
             nc.vector.quantize_mx(
-                out=codes[:, c0 : c0 + cols].bitcast(FP8X4),
-                scales=scales[:, c0 : c0 + cols],
-                in_=grouped[:, c0 : c0 + cols, :].rearrange("p c t -> p (c t)"),
+                out=codes[:, first : first + cols].bitcast(FP8X4),
+                scales=scales[:, first : first + cols],
+                in_=grouped[:, first : first + cols, :].rearrange("p c t -> p (c t)"),
             )
 
-        def word_transposes(src, g0):
-            t = bank("fw", 3, "wt")
-            srcw = src[:].bitcast(F32)
-            for g2 in range(2):
+        def reciprocal_norm(rnorm, clamped, sumsq, first, width):
+            cols = slice(first, first + width)
+            nc.gpsimd.tensor_scalar(
+                out=clamped[:, cols], in0=sumsq[:, cols], scalar1=NORM_EPS_SQUARED, scalar2=None, op0=ALU.max
+            )
+            nc.gpsimd.tensor_tensor(
+                out=rnorm[:, cols], in0=clamped[:, cols], in1=minus_half[:, 0:width], op=ALU.pow
+            )
+
+        def spread(dst, column):
+            nc.tensor.transpose(dst, column.to_broadcast([P, P]), identity[:])
+
+        def words_onto_partitions(src, first):
+            t = bank("kt")
+            words = src[:].bitcast(F32)
+            for i in range(2):
                 for u in range(2):
-                    c0 = 256 * u + 128 * g2
+                    col = 256 * u + P * i
                     nc.tensor.transpose(
-                        t[:, c0 : c0 + 128], srcw[:, g0 + g2, 128 * u : 128 * u + 128], ident_f[:]
+                        t[:, col : col + P], words[:, first + i, P * u : P * u + P], identity[:]
                     )
             return t
 
-        def words_out(dst, src, g0):
-            t = word_transposes(src, g0)
+        def regroup(dst, src, first):
+            t = words_onto_partitions(src, first)
             nc.scalar.copy(
-                out=dst[:].bitcast(F32)[:, 128 * g0 : 128 * g0 + 256, :],
+                out=dst[:].bitcast(F32)[:, P * first : P * first + 256, :],
                 in_=t[:].rearrange("q (u c) -> q c u", u=2),
             )
 
-        def tok_b():
-            words_out(gbias, bias_sb, 0)
-            words_out(gbias, bias_sb, 2)
+        def bias_in():
+            regroup(bias_grouped, bias_sb, 0)
+            regroup(bias_grouped, bias_sb, 2)
 
-        def tok_w():
-            words_out(gw, wc_sb, 0)
-            words_out(gw, wc_sb, 2)
-            quantise(gw, wq, ws, 0, D)
-            cst_ps = bank("fw", 3, "cst_ps", BF16, P)
-            nc.tensor.transpose(cst_ps[:], small[:], ident_b[:])
-            nc.vector.tensor_copy(out=cst[:], in_=cst_ps[:, 0:12])
+        def weights_in():
+            regroup(w_grouped, wc_sb, 0)
+            regroup(w_grouped, wc_sb, 2)
+            quantise(w_grouped, w_codes, w_scales, 0, D)
+            nc.vector.tensor_copy(out=bc_f[:], in_=bc_bf[:])
+            nc.vector.tensor_copy(out=alpha[:], in_=alpha_bf[:])
+            nc.vector.tensor_copy(out=beta[:], in_=beta_bf[:])
 
-        def tok_x(b):
-            ts = [word_transposes(cl_sb, 4 * b + 2 * h) for h in range(2)]
+        def centres_in(b):
+            halves = [words_onto_partitions(cl_sb, G * b + 2 * h) for h in range(2)]
             for h in range(2):
-                g0 = 4 * b + 2 * h
+                first = M * b + 256 * h
                 nc.vector.tensor_tensor(
-                    out=gx[:, 128 * g0 : 128 * g0 + 256, :].rearrange("q c (u e) -> q c u e", u=2),
-                    in0=ts[h][:].bitcast(BF16).rearrange("q (u c e) -> q c u e", u=2, e=2),
-                    in1=gbias[:, 256 * h : 256 * h + 256, :].rearrange("q c (u e) -> q c u e", u=2),
+                    out=x_grouped[:, first : first + 256, :].rearrange("q c (u e) -> q c u e", u=2),
+                    in0=halves[h][:].bitcast(BF16).rearrange("q (u c e) -> q c u e", u=2, e=2),
+                    in1=bias_grouped[:, 256 * h : 256 * h + 256, :].rearrange("q c (u e) -> q c u e", u=2),
                     op=ALU.add,
                 )
-            quantise(gx, xq, xs, M * b, M)
+            quantise(x_grouped, x_codes, x_scales, M * b, M)
 
-        def tok_z(b):
-            for ot in range(4):
-                z = bank("mx", 2, "z")
+        def centres_matmul(b):
+            for t in range(G):
+                z = bank("z")
                 nc.tensor.matmul_mx(
                     out=z[:],
-                    lhsT=wq[:, 128 * ot : 128 * ot + 128].bitcast(FP8X4),
-                    lhsT_scale=ws[:, 128 * ot : 128 * ot + 128],
-                    rhs=xq[:, M * b : M * b + M].bitcast(FP8X4),
-                    rhs_scale=xs[:, M * b : M * b + M],
+                    lhsT=w_codes[:, P * t : P * t + P].bitcast(FP8X4),
+                    lhsT_scale=w_scales[:, P * t : P * t + P],
+                    rhs=x_codes[:, M * b : M * b + M].bitcast(FP8X4),
+                    rhs_scale=x_scales[:, M * b : M * b + M],
                     start=True,
                     stop=True,
                 )
                 nc.scalar.activation(
-                    out=c_sb[:, ot, M * b : M * b + M],
-                    in_=z[:],
-                    func=ACT.Silu,
-                    bias=cst[:, 8 + ot : 9 + ot],
-                    scale=1.0,
+                    out=c_sb[:, t, M * b : M * b + M], in_=z[:], func=ACT.Silu, bias=bc_f[:, t : t + 1], scale=1.0
                 )
 
-        def tok_c_pre(b):
-            for mt in range(4):
-                g = 4 * b + mt
-                ct = bank("fw", 3, "ct")
-                for ot in range(4):
-                    nc.tensor.transpose(
-                        ct[:, 128 * ot : 128 * ot + 128],
-                        c_sb[:, ot, 128 * g : 128 * g + 128],
-                        ident_f[:],
-                    )
+        def centres_norm(b):
+            for g in range(G):
+                first = M * b + P * g
+                ct = bank("ct")
+                for t in range(G):
+                    nc.tensor.transpose(ct[:, P * t : P * t + P], c_sb[:, t, first : first + P], identity[:])
                 nc.scalar.activation(
-                    out=junk[:], in_=ct[:], func=ACT.Square, accum_out=ss_c[:, g : g + 1]
+                    out=squares[:], in_=ct[:], func=ACT.Square, accum_out=c_sumsq[:, G * b + g : G * b + g + 1]
                 )
-            sl = slice(4 * b, 4 * b + 4)
-            nc.gpsimd.tensor_scalar(
-                out=cl_c[:, sl], in0=ss_c[:, sl], scalar1=EPS2, scalar2=None, op0=ALU.max
-            )
-            nc.gpsimd.tensor_tensor(out=rn_c[:, sl], in0=cl_c[:, sl], in1=mhalf[:, 0:4], op=ALU.pow)
+            reciprocal_norm(c_rnorm, c_clamped, c_sumsq, G * b, G)
 
-        def tok_c_post(b):
-            rc = bank("bk", 3, "rc")
-            for mt in range(4):
-                g = 4 * b + mt
-                nc.tensor.transpose(
-                    rc[:, 128 * mt : 128 * mt + 128],
-                    rn_c[:, g : g + 1].to_broadcast([P, P]),
-                    ident_f[:],
-                )
+        def centres_out(b):
+            rn = bank("rn_c")
+            for g in range(G):
+                spread(rn[:, P * g : P * g + P], c_rnorm[:, G * b + g : G * b + g + 1])
             nc.vector.tensor_tensor(
-                out=gc[:, M * b : M * b + M, :],
-                in0=rc[:].unsqueeze(2).to_broadcast([P, M, 4]),
+                out=c_grouped[:, M * b : M * b + M, :],
+                in0=rn[:].unsqueeze(2).to_broadcast([P, M, G]),
                 in1=c_sb[:, :, M * b : M * b + M].rearrange("p t m -> p m t"),
                 op=ALU.mult,
             )
-            quantise(gc, cq, cs, M * b, M)
+            quantise(c_grouped, c_codes, c_scales, M * b, M)
 
-        def tok_f_pre(b, j):
-            bj = 4 * b + j
-            f = bank("fw", 3, "f")
-            for t in range(4):
-                nc.tensor.transpose(
-                    f[:, 128 * t : 128 * t + 128], ptw[:, b, t, 128 * j : 128 * j + 128], ident_f[:]
-                )
-            fb = f[:].bitcast(BF16).rearrange("w (d e) -> w e d", e=2)
+        def points_front(b, j):
+            block = G * b + j
+            f = bank("f")
+            for t in range(G):
+                nc.tensor.transpose(f[:, P * t : P * t + P], pts_words[:, b, t, P * j : P * j + P], identity[:])
+            pairs = f[:].bitcast(BF16).rearrange("w (d e) -> w e d", e=2)
             for e in range(2):
                 nc.scalar.activation(
-                    out=junk[:],
-                    in_=fb[:, e, :],
+                    out=squares[:],
+                    in_=pairs[:, e, :],
                     func=ACT.Square,
-                    accum_out=ss_p[:, 2 * bj + e : 2 * bj + e + 1],
+                    accum_out=p_sumsq[:, 2 * block + e : 2 * block + e + 1],
                 )
-            sl = slice(2 * bj, 2 * bj + 2)
-            nc.gpsimd.tensor_scalar(
-                out=cl_p[:, sl], in0=ss_p[:, sl], scalar1=EPS2, scalar2=None, op0=ALU.max
-            )
-            nc.gpsimd.tensor_tensor(out=rn_p[:, sl], in0=cl_p[:, sl], in1=mhalf[:, 0:2], op=ALU.pow)
+            reciprocal_norm(p_rnorm, p_clamped, p_sumsq, 2 * block, 2)
 
-        def tok_f_post(b, j):
-            bj = 4 * b + j
-            rb = bank("bk", 3, "rb", F32, 256)
+        def points_back(b, j):
+            block = G * b + j
+            rn = bank("rn_p", BLOCK)
             for e in range(2):
-                nc.tensor.transpose(
-                    rb[:, 128 * e : 128 * e + 128],
-                    rn_p[:, 2 * bj + e : 2 * bj + e + 1].to_broadcast([P, P]),
-                    ident_f[:],
-                )
-            n0 = 256 * j
+                spread(rn[:, P * e : P * e + P], p_rnorm[:, 2 * block + e : 2 * block + e + 1])
+            first = BLOCK * j
             nc.vector.tensor_tensor(
-                out=gp[:, N * b + n0 : N * b + n0 + 256, :].rearrange("p (w e) t -> p w e t", e=2),
-                in0=rb[:].rearrange("p (e w) -> p w e", e=2).unsqueeze(3).to_broadcast([P, P, 2, 4]),
-                in1=pts[:, b, :, n0 : n0 + 256].rearrange("p t (w e) -> p w e t", e=2),
+                out=p_grouped[:, N * b + first : N * b + first + BLOCK, :].rearrange("p (w e) t -> p w e t", e=2),
+                in0=rn[:].rearrange("p (e w) -> p w e", e=2).unsqueeze(3).to_broadcast([P, P, 2, G]),
+                in1=pts[:, b, :, first : first + BLOCK].rearrange("p t (w e) -> p w e t", e=2),
                 op=ALU.mult,
             )
             if j % 2 == 1:
-                quantise(gp, pq, pscl, N * b + 256 * (j - 1), 512)
+                quantise(p_grouped, p_codes, p_scales, N * b + first - BLOCK, CHUNK)
 
-        def sim_pass(c, mt):
-            b, h = divmod(c, 2)
-            s = bank("mx", 2, "s")
-            c0 = M * b + 128 * mt
-            n0 = N * b + 512 * h
+        def points_step(i):
+            if i < B * G:
+                points_front(*divmod(i, G))
+            if i >= 2:
+                points_back(*divmod(i - 2, G))
+
+        def similarities(c, g):
+            b, half = divmod(c, 2)
+            s = bank("s")
+            first = M * b + P * g
+            cols = slice(N * b + CHUNK * half, N * b + CHUNK * half + CHUNK)
             nc.tensor.matmul_mx(
                 out=s[:],
-                lhsT=cq[:, c0 : c0 + 128].bitcast(FP8X4),
-                lhsT_scale=cs[:, c0 : c0 + 128],
-                rhs=pq[:, n0 : n0 + 512].bitcast(FP8X4),
-                rhs_scale=pscl[:, n0 : n0 + 512],
+                lhsT=c_codes[:, first : first + P].bitcast(FP8X4),
+                lhsT_scale=c_scales[:, first : first + P],
+                rhs=p_codes[:, cols].bitcast(FP8X4),
+                rhs_scale=p_scales[:, cols],
                 start=True,
                 stop=True,
             )
-            live[("s", c, mt)] = s
+            live["s", c, g] = s
 
-        def logits(c, mt):
-            if mt == 0:
-                live[("l", c)] = work.tile([P, 4, 512], F32, name="lsb", tag="lsb", bufs=2)
+        def logits(c, g):
+            if g == 0:
+                live["l", c] = work.tile([P, G, CHUNK], F32, name="logit", tag="logit", bufs=2)
             nc.scalar.activation(
-                out=live[("l", c)][:, mt, :],
-                in_=live[("s", c, mt)][:],
+                out=live["l", c][:, g, :],
+                in_=live["s", c, g][:],
                 func=ACT.Identity,
-                bias=cst[:, 4 + mt : 5 + mt],
-                scale=cst[:, mt : mt + 1],
+                bias=beta[:, g : g + 1],
+                scale=alpha[:, g : g + 1],
             )
 
-        def fwd(k):
+        def first_logits():
+            for g in range(G):
+                similarities(0, g)
+                logits(0, g)
+
+        def points_onto_partitions(k):
             c, i = divmod(k, 4)
-            lt = bank("fw", 3, "lt")
-            for mt in range(4):
-                nc.tensor.transpose(
-                    lt[:, 128 * mt : 128 * mt + 128],
-                    live[("l", c)][:, mt, 128 * i : 128 * i + 128],
-                    ident_f[:],
-                )
-            live[("lt", k)] = lt
+            lt = bank("lt")
+            for g in range(G):
+                nc.tensor.transpose(lt[:, P * g : P * g + P], live["l", c][:, g, P * i : P * i + P], identity[:])
+            live["lt", k] = lt
 
-        def col_max(k):
-            nmx = work.tile([P, 1], F32, name="nmx", tag="nmx", bufs=6)
-            nc.vector.tensor_reduce(
-                out=nmx[:], in_=live[("lt", k)][:], axis=AX.X, op=ALU.max, negate=True
-            )
-            live[("nmx", k)] = nmx
+        def row_max(k):
+            neg_max = work.tile([P, 1], F32, name="neg_max", tag="neg_max", bufs=6)
+            nc.vector.tensor_reduce(out=neg_max[:], in_=live["lt", k][:], axis=AX.X, op=ALU.max, negate=True)
+            live["max", k] = neg_max
 
-        def col_exp(k):
-            et = work.tile([P, 512], F32, name="et", tag="et", bufs=6)
-            sm = work.tile([P, 1], F32, name="sm", tag="sm", bufs=6)
+        def exponentials(k):
+            ex = work.tile([P, M], F32, name="ex", tag="ex", bufs=8)
+            total = work.tile([P, 1], F32, name="total", tag="total", bufs=6)
             nc.scalar.activation(
-                out=et[:],
-                in_=live[("lt", k)][:],
-                func=ACT.Exp,
-                bias=live[("nmx", k)][:],
-                scale=1.0,
-                accum_out=sm[:],
+                out=ex[:], in_=live["lt", k][:], func=ACT.Exp, bias=live["max", k][:], scale=1.0, accum_out=total[:]
             )
-            live[("et", k)] = et
-            live[("sm", k)] = sm
+            live["ex", k] = ex
+            live["total", k] = total
 
-        def col_scale(k):
-            rs = work.tile([P, 1], F32, name="rs", tag="rs", bufs=6)
-            nc.vector.reciprocal(out=rs[:], in_=live[("sm", k)][:])
-            et = live[("et", k)]
-            nc.vector.tensor_scalar(out=et[:], in0=et[:], scalar1=rs[:], scalar2=None, op0=ALU.mult)
+        def normalise(k):
+            share = work.tile([P, 1], F32, name="share", tag="share", bufs=6)
+            nc.vector.reciprocal(out=share[:], in_=live["total", k][:])
+            ex = live["ex", k]
+            nc.gpsimd.tensor_scalar(out=ex[:], in0=ex[:], scalar1=share[:], scalar2=0.0, op0=ALU.mult, op1=ALU.add)
 
-        def bwd(k):
-            o = bank("bk", 3, "o")
-            et = live[("et", k)]
-            for mt in range(4):
-                nc.tensor.transpose(
-                    o[:, 128 * mt : 128 * mt + 128], et[:, 128 * mt : 128 * mt + 128], ident_f[:]
-                )
-            live[("o", k)] = o
+        def clusters_onto_partitions(k):
+            o = bank("o")
+            for g in range(G):
+                nc.tensor.transpose(o[:, P * g : P * g + P], live["ex", k][:, P * g : P * g + P], identity[:])
+            live["o", k] = o
 
-        def evac(k):
+        def copy_out(k):
             c, i = divmod(k, 4)
             if i == 0:
-                live[("ost", c)] = work.tile([P, 4, 512], F32, name="ost", tag="ost", bufs=2)
-            ost = live[("ost", c)]
-            copy_out = nc.scalar.copy if i == 0 else nc.vector.tensor_copy
-            copy_out(
-                out=ost[:, :, 128 * i : 128 * i + 128],
-                in_=live[("o", k)][:].rearrange("p (t n) -> p t n", t=4),
+                live["out", c] = work.tile([P, G, CHUNK], F32, name="result", tag="result", bufs=2)
+            result = live["out", c]
+            nc.vector.tensor_copy(
+                out=result[:, :, P * i : P * i + P], in_=live["o", k][:].rearrange("p (g n) -> p g n", g=G)
             )
-            b, h = divmod(c, 2)
-            rows = out[b].rearrange("(t p) n -> p t n", p=P)
-            if c == 3:
-                n0 = 512 * h + 128 * i
-                nc.sync.dma_start(out=rows[:, :, n0 : n0 + 128], in_=ost[:, :, 128 * i : 128 * i + 128])
+            b, half = divmod(c, 2)
+            rows = out[b].rearrange("(p g) n -> p g n", g=G)
+            if c == TILES // 4 - 1:
+                first = CHUNK * half + P * i
+                nc.sync.dma_start(out=rows[:, :, first : first + P], in_=result[:, :, P * i : P * i + P])
             elif i == 3:
-                nc.sync.dma_start(out=rows[:, :, 512 * h : 512 * h + 512], in_=ost[:])
+                nc.sync.dma_start(out=rows[:, :, CHUNK * half : CHUNK * half + CHUNK], in_=result[:])
 
-        units = 16
+        def softmax_step(p):
+            if 0 <= p + 1 < TILES:
+                points_onto_partitions(p + 1)
+            if 0 <= p - 6 < TILES:
+                copy_out(p - 6)
+            if 0 <= p < TILES:
+                row_max(p)
+            if 0 <= p - 2 < TILES:
+                normalise(p - 2)
+            c, g = divmod(p + 5, 4)
+            if 1 <= c < TILES // 4:
+                logits(c, g)
+            c, g = divmod(p + 6, 4)
+            if 1 <= c < TILES // 4 and g % 2 == 0:
+                similarities(c, g)
+                similarities(c, g + 1)
+            if 0 <= p < TILES:
+                exponentials(p)
+            if 0 <= p - 4 < TILES:
+                clusters_onto_partitions(p - 4)
 
-        def prologue():
-            for mt in range(4):
-                sim_pass(0, mt)
-                logits(0, mt)
-
-        def step(p):
-            if 0 <= p + 1 < units:
-                fwd(p + 1)
-            if 0 <= p - 5 < units:
-                evac(p - 5)
-            if 0 <= p < units:
-                col_max(p)
-            if 0 <= p - 1 < units:
-                col_scale(p - 1)
-            for c in range(1, 4):
-                for mt in range(4):
-                    if p == 4 * (c - 1) + mt - 1:
-                        logits(c, mt)
-            for c in range(1, 4):
-                if p == 4 * (c - 1) - 2:
-                    sim_pass(c, 0)
-                    sim_pass(c, 1)
-                if p == 4 * (c - 1):
-                    sim_pass(c, 2)
-                    sim_pass(c, 3)
-            if 0 <= p < units:
-                col_exp(p)
-            if 0 <= p - 3 < units:
-                bwd(p - 3)
-
-        def keep_clock():
-            scratch = bank("ps", 8, "scratch")
-            for i in range(2):
-                nc.tensor.matmul_mx(
-                    out=scratch[:],
-                    lhsT=wq[:, 0:128].bitcast(FP8X4),
-                    lhsT_scale=ws[:, 0:128],
-                    rhs=wq[:, 0:512].bitcast(FP8X4),
-                    rhs_scale=ws[:, 0:512],
-                    start=True,
-                    stop=True,
-                )
-
-        todo = {
-            "D": (keep_clock,),
-            "B": (tok_b,),
-            "W": (tok_w,),
-            "P": (prologue,),
-        }
-        for b in range(B):
-            todo["X%d" % b] = (tok_x, b)
-            todo["Z%d" % b] = (tok_z, b)
-            todo["C%d" % b] = (tok_c_pre, b)
-            todo["c%d" % b] = (tok_c_post, b)
-            for j in range(4):
-                todo["F%d%d" % (b, j)] = (tok_f_pre, b, j)
-                todo["f%d%d" % (b, j)] = (tok_f_post, b, j)
-        order = [
-            "B", "X0", "W", "F00", "F01", "Z0", "F10", "f00", "X1", "F02", "f01", "C0", "F11", "f10", "Z1", "f02", "c0", "F03", "D", "C1", "f11", "F12", "f03", "P", "F13", "c1", "T", "T", "T", "f12", "T", "f13", "T", "D", "T", "D", "T", "T", "T", "T", "T", "T", "T", "T", "T", "T", "T", "D", "T", "T", "T", "T", "T", "T",
-        ]
-        p = -2
-        for name in order:
-            if name == "T":
-                step(p)
-                p += 1
-            else:
-                todo[name][0](*todo[name][1:])
-        assert p == units + 5
+        bias_in()
+        centres_in(0)
+        weights_in()
+        points_step(0)
+        points_step(1)
+        centres_matmul(0)
+        points_step(2)
+        centres_in(1)
+        points_step(3)
+        centres_norm(0)
+        points_step(4)
+        centres_matmul(1)
+        points_step(5)
+        centres_out(0)
+        points_step(6)
+        centres_norm(1)
+        points_step(7)
+        first_logits()
+        points_step(8)
+        centres_out(1)
+        points_step(9)
+        for p in range(-2, TILES + 6):
+            softmax_step(p)

@@ -16,8 +16,14 @@ P = 128
 G = 4
 B, M, D, N = 2, 512, 512, 1024
 CHUNK = 512
+CHUNKS_PER_BATCH = N // CHUNK
+CHUNKS = B * CHUNKS_PER_BATCH
 BLOCK = 256
+BLOCKS_PER_BATCH = N // BLOCK
+BLOCKS = B * BLOCKS_PER_BATCH
 TILES = B * N // P
+TILES_PER_CHUNK = CHUNK // P
+PAIR = 2 * P
 FLOPS = 2 * B * M * D * D + 2 * B * M * D * N
 NORM_EPS_SQUARED = 1e-24
 
@@ -61,8 +67,8 @@ def tile_fuzzyclustering_pa_kernel(
         load_clusters(0)
         nc.sync.dma_start(out=wc_sb[:], in_=Wc.rearrange("(p g) k -> p g k", g=G))
         load_points(0, 0)
-        load_clusters(1)
         load_points(0, 1)
+        load_clusters(1)
         load_points(1, 0)
         load_points(1, 1)
 
@@ -96,9 +102,9 @@ def tile_fuzzyclustering_pa_kernel(
         c_sumsq = keep.tile([P, B * G], F32, name="c_sumsq")
         c_clamped = keep.tile([P, B * G], F32, name="c_clamped")
         c_rnorm = keep.tile([P, B * G], F32, name="c_rnorm")
-        p_sumsq = keep.tile([P, 2 * B * G], F32, name="p_sumsq")
-        p_clamped = keep.tile([P, 2 * B * G], F32, name="p_clamped")
-        p_rnorm = keep.tile([P, 2 * B * G], F32, name="p_rnorm")
+        p_sumsq = keep.tile([P, 2 * BLOCKS], F32, name="p_sumsq")
+        p_clamped = keep.tile([P, 2 * BLOCKS], F32, name="p_clamped")
+        p_rnorm = keep.tile([P, 2 * BLOCKS], F32, name="p_rnorm")
         pts_words = pts[:].bitcast(F32)
         live = {}
 
@@ -122,21 +128,21 @@ def tile_fuzzyclustering_pa_kernel(
             nc.tensor.transpose(dst, column.to_broadcast([P, P]), identity[:])
 
         def words_onto_partitions(src, first):
-            t = bank("kt")
+            kt = bank("kt")
             words = src[:].bitcast(F32)
-            for i in range(2):
+            for side in range(2):
                 for u in range(2):
-                    col = 256 * u + P * i
+                    col = PAIR * u + P * side
                     nc.tensor.transpose(
-                        t[:, col : col + P], words[:, first + i, P * u : P * u + P], identity[:]
+                        kt[:, col : col + P], words[:, first + side, P * u : P * u + P], identity[:]
                     )
-            return t
+            return kt
 
         def regroup(dst, src, first):
-            t = words_onto_partitions(src, first)
+            kt = words_onto_partitions(src, first)
             nc.scalar.copy(
-                out=dst[:].bitcast(F32)[:, P * first : P * first + 256, :],
-                in_=t[:].rearrange("q (u c) -> q c u", u=2),
+                out=dst[:].bitcast(F32)[:, P * first : P * first + PAIR, :],
+                in_=kt[:].rearrange("q (u c) -> q c u", u=2),
             )
 
         def bias_in():
@@ -154,11 +160,11 @@ def tile_fuzzyclustering_pa_kernel(
         def centres_in(b):
             halves = [words_onto_partitions(cl_sb, G * b + 2 * h) for h in range(2)]
             for h in range(2):
-                first = M * b + 256 * h
+                first = M * b + PAIR * h
                 nc.vector.tensor_tensor(
-                    out=x_grouped[:, first : first + 256, :].rearrange("q c (u e) -> q c u e", u=2),
+                    out=x_grouped[:, first : first + PAIR, :].rearrange("q c (u e) -> q c u e", u=2),
                     in0=halves[h][:].bitcast(BF16).rearrange("q (u c e) -> q c u e", u=2, e=2),
-                    in1=bias_grouped[:, 256 * h : 256 * h + 256, :].rearrange("q c (u e) -> q c u e", u=2),
+                    in1=bias_grouped[:, PAIR * h : PAIR * h + PAIR, :].rearrange("q c (u e) -> q c u e", u=2),
                     op=ALU.add,
                 )
             quantise(x_grouped, x_codes, x_scales, M * b, M)
@@ -203,7 +209,7 @@ def tile_fuzzyclustering_pa_kernel(
             quantise(c_grouped, c_codes, c_scales, M * b, M)
 
         def points_front(b, j):
-            block = G * b + j
+            block = BLOCKS_PER_BATCH * b + j
             f = bank("f")
             for t in range(G):
                 nc.tensor.transpose(f[:, P * t : P * t + P], pts_words[:, b, t, P * j : P * j + P], identity[:])
@@ -218,7 +224,7 @@ def tile_fuzzyclustering_pa_kernel(
             reciprocal_norm(p_rnorm, p_clamped, p_sumsq, 2 * block, 2)
 
         def points_back(b, j):
-            block = G * b + j
+            block = BLOCKS_PER_BATCH * b + j
             rn = bank("rn_p", BLOCK)
             for e in range(2):
                 spread(rn[:, P * e : P * e + P], p_rnorm[:, 2 * block + e : 2 * block + e + 1])
@@ -232,14 +238,14 @@ def tile_fuzzyclustering_pa_kernel(
             if j % 2 == 1:
                 quantise(p_grouped, p_codes, p_scales, N * b + first - BLOCK, CHUNK)
 
-        def points_step(i):
-            if i < B * G:
-                points_front(*divmod(i, G))
-            if i >= 2:
-                points_back(*divmod(i - 2, G))
+        def points_step(step):
+            if step < BLOCKS:
+                points_front(*divmod(step, BLOCKS_PER_BATCH))
+            if step >= 2:
+                points_back(*divmod(step - 2, BLOCKS_PER_BATCH))
 
-        def similarities(c, g):
-            b, half = divmod(c, 2)
+        def similarities(chunk, g):
+            b, half = divmod(chunk, CHUNKS_PER_BATCH)
             s = bank("s")
             first = M * b + P * g
             cols = slice(N * b + CHUNK * half, N * b + CHUNK * half + CHUNK)
@@ -252,14 +258,14 @@ def tile_fuzzyclustering_pa_kernel(
                 start=True,
                 stop=True,
             )
-            live["s", c, g] = s
+            live["s", chunk, g] = s
 
-        def logits(c, g):
+        def logits(chunk, g):
             if g == 0:
-                live["l", c] = work.tile([P, G, CHUNK], F32, name="logit", tag="logit", bufs=2)
+                live["l", chunk] = work.tile([P, G, CHUNK], F32, name="logit", tag="logit", bufs=2)
             nc.scalar.activation(
-                out=live["l", c][:, g, :],
-                in_=live["s", c, g][:],
+                out=live["l", chunk][:, g, :],
+                in_=live["s", chunk, g][:],
                 func=ACT.Identity,
                 bias=beta[:, g : g + 1],
                 scale=alpha[:, g : g + 1],
@@ -271,10 +277,12 @@ def tile_fuzzyclustering_pa_kernel(
                 logits(0, g)
 
         def points_onto_partitions(k):
-            c, i = divmod(k, 4)
+            chunk, quarter = divmod(k, TILES_PER_CHUNK)
             lt = bank("lt")
             for g in range(G):
-                nc.tensor.transpose(lt[:, P * g : P * g + P], live["l", c][:, g, P * i : P * i + P], identity[:])
+                nc.tensor.transpose(
+                    lt[:, P * g : P * g + P], live["l", chunk][:, g, P * quarter : P * quarter + P], identity[:]
+                )
             live["lt", k] = lt
 
         def row_max(k):
@@ -295,7 +303,12 @@ def tile_fuzzyclustering_pa_kernel(
             share = work.tile([P, 1], F32, name="share", tag="share", bufs=6)
             nc.vector.reciprocal(out=share[:], in_=live["total", k][:])
             ex = live["ex", k]
-            nc.gpsimd.tensor_scalar(out=ex[:], in0=ex[:], scalar1=share[:], scalar2=0.0, op0=ALU.mult, op1=ALU.add)
+            if k < TILES - 2:
+                nc.gpsimd.tensor_scalar(
+                    out=ex[:], in0=ex[:], scalar1=share[:], scalar2=0.0, op0=ALU.mult, op1=ALU.add
+                )
+            else:
+                nc.vector.tensor_scalar(out=ex[:], in0=ex[:], scalar1=share[:], scalar2=None, op0=ALU.mult)
 
         def clusters_onto_partitions(k):
             o = bank("o")
@@ -304,41 +317,40 @@ def tile_fuzzyclustering_pa_kernel(
             live["o", k] = o
 
         def copy_out(k):
-            c, i = divmod(k, 4)
-            if i == 0:
-                live["out", c] = work.tile([P, G, CHUNK], F32, name="result", tag="result", bufs=2)
-            result = live["out", c]
-            nc.vector.tensor_copy(
-                out=result[:, :, P * i : P * i + P], in_=live["o", k][:].rearrange("p (g n) -> p g n", g=G)
-            )
-            b, half = divmod(c, 2)
+            chunk, quarter = divmod(k, TILES_PER_CHUNK)
+            if quarter == 0:
+                live["out", chunk] = work.tile([P, G, CHUNK], F32, name="result", tag="result", bufs=2)
+            result = live["out", chunk]
+            cols = slice(P * quarter, P * quarter + P)
+            nc.vector.tensor_copy(out=result[:, :, cols], in_=live["o", k][:].rearrange("p (g n) -> p g n", g=G))
+            b, half = divmod(chunk, CHUNKS_PER_BATCH)
             rows = out[b].rearrange("(p g) n -> p g n", g=G)
-            if c == TILES // 4 - 1:
-                first = CHUNK * half + P * i
-                nc.sync.dma_start(out=rows[:, :, first : first + P], in_=result[:, :, P * i : P * i + P])
-            elif i == 3:
-                nc.sync.dma_start(out=rows[:, :, CHUNK * half : CHUNK * half + CHUNK], in_=result[:])
+            first = CHUNK * half
+            if chunk == CHUNKS - 1:
+                nc.sync.dma_start(out=rows[:, :, first + P * quarter : first + P * quarter + P], in_=result[:, :, cols])
+            elif quarter == TILES_PER_CHUNK - 1:
+                nc.sync.dma_start(out=rows[:, :, first : first + CHUNK], in_=result[:])
 
-        def softmax_step(p):
-            if 0 <= p + 1 < TILES:
-                points_onto_partitions(p + 1)
-            if 0 <= p - 6 < TILES:
-                copy_out(p - 6)
-            if 0 <= p < TILES:
-                row_max(p)
-            if 0 <= p - 2 < TILES:
-                normalise(p - 2)
-            c, g = divmod(p + 5, 4)
-            if 1 <= c < TILES // 4:
-                logits(c, g)
-            c, g = divmod(p + 6, 4)
-            if 1 <= c < TILES // 4 and g % 2 == 0:
-                similarities(c, g)
-                similarities(c, g + 1)
-            if 0 <= p < TILES:
-                exponentials(p)
-            if 0 <= p - 4 < TILES:
-                clusters_onto_partitions(p - 4)
+        def softmax_step(step):
+            if 0 <= step + 1 < TILES:
+                points_onto_partitions(step + 1)
+            if 0 <= step - 6 < TILES:
+                copy_out(step - 6)
+            if 0 <= step < TILES:
+                row_max(step)
+            if 0 <= step - 2 < TILES:
+                normalise(step - 2)
+            chunk, g = divmod(step + 5, G)
+            if 1 <= chunk < CHUNKS:
+                logits(chunk, g)
+            chunk, g = divmod(step + 6, G)
+            if 1 <= chunk < CHUNKS and g % 2 == 0:
+                similarities(chunk, g)
+                similarities(chunk, g + 1)
+            if 0 <= step < TILES:
+                exponentials(step)
+            if 0 <= step - 4 < TILES:
+                clusters_onto_partitions(step - 4)
 
         bias_in()
         centres_in(0)
@@ -360,6 +372,8 @@ def tile_fuzzyclustering_pa_kernel(
         first_logits()
         points_step(8)
         centres_out(1)
+        for step in range(-2, 2):
+            softmax_step(step)
         points_step(9)
-        for p in range(-2, TILES + 6):
-            softmax_step(p)
+        for step in range(2, TILES + 6):
+            softmax_step(step)

@@ -21,6 +21,7 @@ CHUNKS = B * CHUNKS_PER_BATCH
 BLOCK = 256
 BLOCKS_PER_BATCH = N // BLOCK
 BLOCKS = B * BLOCKS_PER_BATCH
+GRAM = (0, 3)
 TILES = B * N // P
 TILES_PER_CHUNK = CHUNK // P
 PAIR = 2 * P
@@ -63,9 +64,9 @@ def tile_fuzzyclustering_pa_kernel(
                 out=pts[:, b, :, cols], in_=points[b].rearrange("(p t) n -> p t n", t=G)[:, :, cols]
             )
 
+        nc.sync.dma_start(out=wc_sb[:], in_=Wc.rearrange("(p g) k -> p g k", g=G))
         nc.sync.dma_start(out=bias_sb[:], in_=clusters_bias.rearrange("(p g) k -> p g k", g=G))
         load_clusters(0)
-        nc.sync.dma_start(out=wc_sb[:], in_=Wc.rearrange("(p g) k -> p g k", g=G))
         load_points(0, 0)
         load_points(0, 1)
         load_clusters(1)
@@ -84,7 +85,7 @@ def tile_fuzzyclustering_pa_kernel(
         alpha = keep.tile([P, G], F32, name="alpha")
         beta = keep.tile([P, G], F32, name="beta")
         bc_f = keep.tile([P, G], F32, name="bc_f")
-        bias_grouped = keep.tile([P, M, G], BF16, name="bias_grouped", align_bytes=64)
+        x_rows = keep.tile([P, B * G, D], BF16, name="x_rows")
         w_grouped = keep.tile([P, D, G], BF16, name="w_grouped", align_bytes=64)
         x_grouped = keep.tile([P, B * M, G], BF16, name="x_grouped", align_bytes=64)
         c_grouped = keep.tile([P, B * M, G], BF16, name="c_grouped", align_bytes=64)
@@ -98,6 +99,7 @@ def tile_fuzzyclustering_pa_kernel(
         p_codes = keep.tile([P, B * N], U32, name="p_codes", align_bytes=64)
         p_scales = keep.tile([P, B * N], U8, name="p_scales", align_bytes=64)
         c_sb = keep.tile([P, G, B * M], F32, name="c_sb")
+        diagonal = keep.tile([P, P], BF16, name="diagonal")
         squares = keep.tile([P, CHUNK], BF16, name="squares")
         c_sumsq = keep.tile([P, B * G], F32, name="c_sumsq")
         c_clamped = keep.tile([P, B * G], F32, name="c_clamped")
@@ -138,111 +140,177 @@ def tile_fuzzyclustering_pa_kernel(
                     )
             return kt
 
-        def regroup(dst, src, first):
-            kt = words_onto_partitions(src, first)
-            nc.scalar.copy(
-                out=dst[:].bitcast(F32)[:, P * first : P * first + PAIR, :],
-                in_=kt[:].rearrange("q (u c) -> q c u", u=2),
+        def regroup(dst, offset, key, copy):
+            copy(
+                out=dst[:].bitcast(F32)[:, offset : offset + PAIR, :],
+                in_=live[key][:].rearrange("q (u c) -> q c u", u=2),
             )
 
-        def bias_in():
-            regroup(bias_grouped, bias_sb, 0)
-            regroup(bias_grouped, bias_sb, 2)
+        def weights_turn(h):
+            live["w", h] = words_onto_partitions(wc_sb, 2 * h)
 
-        def weights_in():
-            regroup(w_grouped, wc_sb, 0)
-            regroup(w_grouped, wc_sb, 2)
+        def weights_regroup(h, copy):
+            regroup(w_grouped, PAIR * h, ("w", h), copy)
+
+        def weights_quantise():
             quantise(w_grouped, w_codes, w_scales, 0, D)
+
+        def small_in():
             nc.vector.tensor_copy(out=bc_f[:], in_=bc_bf[:])
             nc.vector.tensor_copy(out=alpha[:], in_=alpha_bf[:])
             nc.vector.tensor_copy(out=beta[:], in_=beta_bf[:])
 
-        def centres_in(b):
-            halves = [words_onto_partitions(cl_sb, G * b + 2 * h) for h in range(2)]
-            for h in range(2):
-                first = M * b + PAIR * h
-                nc.vector.tensor_tensor(
-                    out=x_grouped[:, first : first + PAIR, :].rearrange("q c (u e) -> q c u e", u=2),
-                    in0=halves[h][:].bitcast(BF16).rearrange("q (u c e) -> q c u e", u=2, e=2),
-                    in1=bias_grouped[:, PAIR * h : PAIR * h + PAIR, :].rearrange("q c (u e) -> q c u e", u=2),
-                    op=ALU.add,
-                )
-            quantise(x_grouped, x_codes, x_scales, M * b, M)
+        def centres_add(b, h):
+            rows = slice(G * b + 2 * h, G * b + 2 * h + 2)
+            nc.vector.tensor_tensor(
+                out=x_rows[:, rows, :], in0=cl_sb[:, rows, :], in1=bias_sb[:, 2 * h : 2 * h + 2, :], op=ALU.add
+            )
 
-        def centres_matmul(b):
+        def centres_turn(b, h):
+            live["x", b, h] = words_onto_partitions(x_rows, G * b + 2 * h)
+
+        def centres_regroup(b, h, copy):
+            regroup(x_grouped, M * b + PAIR * h, ("x", b, h), copy)
+
+        def centres_in_quantise(b, h):
+            quantise(x_grouped, x_codes, x_scales, M * b + PAIR * h, PAIR)
+
+        def centres_matmul(b, h):
+            cols = slice(M * b + PAIR * h, M * b + PAIR * h + PAIR)
             for t in range(G):
-                z = bank("z")
+                z = bank("z", PAIR)
                 nc.tensor.matmul_mx(
                     out=z[:],
                     lhsT=w_codes[:, P * t : P * t + P].bitcast(FP8X4),
                     lhsT_scale=w_scales[:, P * t : P * t + P],
-                    rhs=x_codes[:, M * b : M * b + M].bitcast(FP8X4),
-                    rhs_scale=x_scales[:, M * b : M * b + M],
+                    rhs=x_codes[:, cols].bitcast(FP8X4),
+                    rhs_scale=x_scales[:, cols],
                     start=True,
                     stop=True,
                 )
                 nc.scalar.activation(
-                    out=c_sb[:, t, M * b : M * b + M], in_=z[:], func=ACT.Silu, bias=bc_f[:, t : t + 1], scale=1.0
+                    out=c_sb[:, t, cols], in_=z[:], func=ACT.Silu, bias=bc_f[:, t : t + 1], scale=1.0
                 )
 
-        def centres_norm(b):
-            for g in range(G):
-                first = M * b + P * g
-                ct = bank("ct")
-                for t in range(G):
-                    nc.tensor.transpose(ct[:, P * t : P * t + P], c_sb[:, t, first : first + P], identity[:])
-                nc.scalar.activation(
-                    out=squares[:], in_=ct[:], func=ACT.Square, accum_out=c_sumsq[:, G * b + g : G * b + g + 1]
-                )
-            reciprocal_norm(c_rnorm, c_clamped, c_sumsq, G * b, G)
+        def centres_turn_back(b, g):
+            first = M * b + P * g
+            ct = bank("ct")
+            for t in range(G):
+                nc.tensor.transpose(ct[:, P * t : P * t + P], c_sb[:, t, first : first + P], identity[:])
+            live["ct", b, g] = ct
 
-        def centres_out(b):
-            rn = bank("rn_c")
-            for g in range(G):
-                spread(rn[:, P * g : P * g + P], c_rnorm[:, G * b + g : G * b + g + 1])
+        def centres_squares(b, g):
+            col = G * b + g
+            nc.scalar.activation(
+                out=squares[:], in_=live["ct", b, g][:], func=ACT.Square, accum_out=c_sumsq[:, col : col + 1]
+            )
+            if g % 2 == 1:
+                reciprocal_norm(c_rnorm, c_clamped, c_sumsq, col - 1, 2)
+
+        def centres_spread(b, h):
+            rn = bank("rn_c", PAIR)
+            for side in range(2):
+                col = G * b + 2 * h + side
+                spread(rn[:, P * side : P * side + P], c_rnorm[:, col : col + 1])
+            live["rn_c", b, h] = rn
+
+        def centres_scale(b, h):
+            cols = slice(M * b + PAIR * h, M * b + PAIR * h + PAIR)
             nc.vector.tensor_tensor(
-                out=c_grouped[:, M * b : M * b + M, :],
-                in0=rn[:].unsqueeze(2).to_broadcast([P, M, G]),
-                in1=c_sb[:, :, M * b : M * b + M].rearrange("p t m -> p m t"),
+                out=c_grouped[:, cols, :],
+                in0=live["rn_c", b, h][:].unsqueeze(2).to_broadcast([P, PAIR, G]),
+                in1=c_sb[:, :, cols].rearrange("p t m -> p m t"),
                 op=ALU.mult,
             )
-            quantise(c_grouped, c_codes, c_scales, M * b, M)
 
-        def points_front(b, j):
-            block = BLOCKS_PER_BATCH * b + j
+        def centres_quantise(b, h):
+            quantise(c_grouped, c_codes, c_scales, M * b + PAIR * h, PAIR)
+
+        def points_norm(chunk):
+            reciprocal_norm(p_rnorm, p_clamped, p_sumsq, G * chunk, G)
+
+        def points_gram(chunk, j):
+            b, half = divmod(chunk, CHUNKS_PER_BATCH)
+            if j == 0:
+                live["gram", chunk] = bank("gram")
+            cols = slice(CHUNK * half + P * j, CHUNK * half + P * j + P)
+            for t in range(G):
+                nc.tensor.matmul(
+                    live["gram", chunk][:, P * j : P * j + P],
+                    lhsT=pts[:, b, t, cols],
+                    rhs=pts[:, b, t, cols],
+                    start=t == 0,
+                    stop=t == G - 1,
+                )
+
+        def points_diagonal(chunk, j):
+            nc.vector.scalar_tensor_tensor(
+                out=diagonal[:],
+                in0=live["gram", chunk][:, P * j : P * j + P],
+                scalar=1.0,
+                in1=identity[:],
+                op0=ALU.mult,
+                op1=ALU.mult,
+                accum_out=p_sumsq[:, G * chunk + j : G * chunk + j + 1],
+            )
+            if j == TILES_PER_CHUNK - 1:
+                points_norm(chunk)
+
+        def points_turn(chunk, j):
+            b, half = divmod(chunk, CHUNKS_PER_BATCH)
+            first = CHUNK * half // 2 + P * j
             f = bank("f")
             for t in range(G):
-                nc.tensor.transpose(f[:, P * t : P * t + P], pts_words[:, b, t, P * j : P * j + P], identity[:])
-            pairs = f[:].bitcast(BF16).rearrange("w (d e) -> w e d", e=2)
+                nc.tensor.transpose(f[:, P * t : P * t + P], pts_words[:, b, t, first : first + P], identity[:])
+            live["f", chunk, j] = f
+
+        def points_squares(chunk, j):
+            pairs = live["f", chunk, j][:].bitcast(BF16).rearrange("w (d e) -> w e d", e=2)
             for e in range(2):
+                col = G * chunk + 2 * j + e
                 nc.scalar.activation(
-                    out=squares[:],
-                    in_=pairs[:, e, :],
-                    func=ACT.Square,
-                    accum_out=p_sumsq[:, 2 * block + e : 2 * block + e + 1],
+                    out=squares[:], in_=pairs[:, e, :], func=ACT.Square, accum_out=p_sumsq[:, col : col + 1]
                 )
-            reciprocal_norm(p_rnorm, p_clamped, p_sumsq, 2 * block, 2)
+            if j == 1:
+                points_norm(chunk)
 
-        def points_back(b, j):
-            block = BLOCKS_PER_BATCH * b + j
-            rn = bank("rn_p", BLOCK)
-            for e in range(2):
-                spread(rn[:, P * e : P * e + P], p_rnorm[:, 2 * block + e : 2 * block + e + 1])
-            first = BLOCK * j
-            nc.vector.tensor_tensor(
-                out=p_grouped[:, N * b + first : N * b + first + BLOCK, :].rearrange("p (w e) t -> p w e t", e=2),
-                in0=rn[:].rearrange("p (e w) -> p w e", e=2).unsqueeze(3).to_broadcast([P, P, 2, G]),
-                in1=pts[:, b, :, first : first + BLOCK].rearrange("p t (w e) -> p w e t", e=2),
-                op=ALU.mult,
-            )
-            if j % 2 == 1:
-                quantise(p_grouped, p_codes, p_scales, N * b + first - BLOCK, CHUNK)
+        def points_spread(chunk):
+            rn = bank("rn_p")
+            for col in range(G):
+                spread(rn[:, P * col : P * col + P], p_rnorm[:, G * chunk + col : G * chunk + col + 1])
+            live["rn_p", chunk] = rn
 
-        def points_step(step):
-            if step < BLOCKS:
-                points_front(*divmod(step, BLOCKS_PER_BATCH))
-            if step >= 2:
-                points_back(*divmod(step - 2, BLOCKS_PER_BATCH))
+        def points_spread_copy(chunk):
+            rn = work.tile([P, CHUNK], F32, name="rn_sb", tag="rn_sb", bufs=2)
+            nc.scalar.copy(out=rn[:], in_=live["rn_p", chunk][:])
+            live["rn_p", chunk] = rn
+
+        def points_scale(chunk, first, width, engine):
+            b, half = divmod(chunk, CHUNKS_PER_BATCH)
+            rn = live["rn_p", chunk]
+            dst = p_grouped[:, CHUNK * chunk + first : CHUNK * chunk + first + width, :]
+            src = pts[:, b, :, CHUNK * half + first : CHUNK * half + first + width]
+            if chunk in GRAM:
+                engine.tensor_tensor(
+                    out=dst,
+                    in0=rn[:, first : first + width].unsqueeze(2).to_broadcast([P, width, G]),
+                    in1=src.rearrange("p t n -> p n t"),
+                    op=ALU.mult,
+                )
+            else:
+                block, inner = divmod(first, BLOCK)
+                factors = rn[:, BLOCK * block : BLOCK * block + BLOCK].rearrange("p (e w) -> p w e", e=2)
+                factors = factors[:, inner // 2 : (inner + width) // 2, :]
+                engine.tensor_tensor(
+                    out=dst.rearrange("p (w e) t -> p w e t", e=2),
+                    in0=factors.unsqueeze(3).to_broadcast([P, width // 2, 2, G]),
+                    in1=src.rearrange("p t (w e) -> p w e t", e=2),
+                    op=ALU.mult,
+                )
+
+        def points_quantise(chunk):
+            b, half = divmod(chunk, CHUNKS_PER_BATCH)
+            quantise(p_grouped, p_codes, p_scales, N * b + CHUNK * half, CHUNK)
 
         def similarities(chunk, g):
             b, half = divmod(chunk, CHUNKS_PER_BATCH)
@@ -352,28 +420,109 @@ def tile_fuzzyclustering_pa_kernel(
             if 0 <= step - 4 < TILES:
                 clusters_onto_partitions(step - 4)
 
-        bias_in()
-        centres_in(0)
-        weights_in()
-        points_step(0)
-        points_step(1)
-        centres_matmul(0)
-        points_step(2)
-        centres_in(1)
-        points_step(3)
-        centres_norm(0)
-        points_step(4)
-        centres_matmul(1)
-        points_step(5)
-        centres_out(0)
-        points_step(6)
-        centres_norm(1)
-        points_step(7)
-        first_logits()
-        points_step(8)
-        centres_out(1)
-        for step in range(-2, 2):
+        sc, vc = nc.scalar.copy, nc.vector.tensor_copy
+        ve = nc.vector
+        weights_turn(0)
+        weights_turn(1)
+        weights_regroup(0, sc)
+        weights_regroup(1, sc)
+        small_in()
+        centres_add(0, 0)
+        centres_add(0, 1)
+        weights_quantise()
+        centres_turn(0, 0)
+        centres_turn(0, 1)
+        points_gram(0, 0)
+        points_gram(0, 1)
+        centres_regroup(0, 0, sc)
+        centres_regroup(0, 1, sc)
+        points_diagonal(0, 0)
+        points_diagonal(0, 1)
+        centres_in_quantise(0, 0)
+        centres_in_quantise(0, 1)
+        points_turn(1, 0)
+        points_squares(1, 0)
+        points_gram(0, 2)
+        points_gram(0, 3)
+        centres_matmul(0, 0)
+        points_diagonal(0, 2)
+        points_diagonal(0, 3)
+        centres_add(1, 0)
+        centres_add(1, 1)
+        centres_matmul(0, 1)
+        centres_turn(1, 0)
+        centres_turn(1, 1)
+        centres_regroup(1, 0, vc)
+        centres_regroup(1, 1, vc)
+        centres_turn_back(0, 0)
+        centres_turn_back(0, 1)
+        centres_squares(0, 0)
+        centres_squares(0, 1)
+        points_gram(3, 0)
+        points_gram(3, 1)
+        centres_turn_back(0, 2)
+        centres_turn_back(0, 3)
+        centres_squares(0, 2)
+        centres_squares(0, 3)
+        points_diagonal(3, 0)
+        centres_in_quantise(1, 0)
+        points_diagonal(3, 1)
+        centres_in_quantise(1, 1)
+        points_turn(1, 1)
+        points_squares(1, 1)
+        centres_matmul(1, 0)
+        points_gram(3, 2)
+        points_gram(3, 3)
+        points_spread(0)
+        points_diagonal(3, 2)
+        points_scale(0, 0, 256, ve)
+        points_diagonal(3, 3)
+        points_scale(0, 256, 256, ve)
+        centres_matmul(1, 1)
+        centres_spread(0, 0)
+        centres_scale(0, 0)
+        points_quantise(0)
+        points_turn(2, 0)
+        centres_spread(0, 1)
+        centres_scale(0, 1)
+        centres_quantise(0, 0)
+        points_squares(2, 0)
+        centres_turn_back(1, 0)
+        centres_turn_back(1, 1)
+        centres_squares(1, 0)
+        centres_squares(1, 1)
+        points_spread(1)
+        points_scale(1, 0, 256, ve)
+        centres_quantise(0, 1)
+        centres_turn_back(1, 2)
+        centres_turn_back(1, 3)
+        centres_squares(1, 2)
+        centres_squares(1, 3)
+        points_turn(2, 1)
+        points_spread(3)
+        points_squares(2, 1)
+        points_spread_copy(3)
+        for first in range(0, 512, 128):
+            points_scale(3, first, 128, nc.gpsimd)
+        for g in range(G):
+            similarities(0, g)
+        points_scale(1, 256, 256, ve)
+        for g in range(G):
+            logits(0, g)
+        points_quantise(1)
+        centres_spread(1, 0)
+        centres_scale(1, 0)
+        centres_spread(1, 1)
+        centres_scale(1, 1)
+        centres_quantise(1, 0)
+        centres_quantise(1, 1)
+        between = {
+            -1: lambda: (points_spread(2), points_scale(2, 0, 256, ve)),
+            0: lambda: points_scale(2, 256, 256, ve),
+            1: lambda: points_quantise(2),
+            5: lambda: points_quantise(3),
+        }
+        for step in range(-2, TILES + 6):
             softmax_step(step)
-        points_step(9)
-        for step in range(2, TILES + 6):
-            softmax_step(step)
+            if step in between:
+                between[step]()

@@ -21,7 +21,10 @@ CHUNKS = B * CHUNKS_PER_BATCH
 BLOCK = 256
 BLOCKS_PER_BATCH = N // BLOCK
 BLOCKS = B * BLOCKS_PER_BATCH
-GRAM = (0, 3)
+GRAM = (1, 2, 3, 4)
+SIMILARITIES_IN = {-2: ((1, 0), (1, 1)), 1: ((1, 2), (1, 3)), 4: ((2, 0), (2, 1)), 5: ((2, 2), (2, 3)), 7: ((3, 0), (3, 1)), 9: ((3, 2), (3, 3))}
+LOGITS_IN = {0: ((1, 0),), 1: ((1, 1),), 2: ((1, 2),(1, 3)), 5: ((2, 0), (2, 1)), 6: ((2, 2), (2, 3)), 8: ((3, 0),), 9: ((3, 1),), 10: ((3, 2), (3, 3))}
+SCALAR_COPIES = (5, 7, 9, 11, 13, 15)
 TILES = B * N // P
 TILES_PER_CHUNK = CHUNK // P
 PAIR = 2 * P
@@ -42,6 +45,9 @@ def tile_fuzzyclustering_pa_kernel(
         def bank(name, width=CHUNK):
             return psum.tile([P, width], F32, tag="bank", name=name)
 
+        def factor_bank(name, width):
+            return psum.tile([P, width], F32, tag="bank", name=name)
+
         alpha_bf = keep.tile([P, G], BF16, name="alpha_bf")
         beta_bf = keep.tile([P, G], BF16, name="beta_bf")
         bc_bf = keep.tile([P, G], BF16, name="bc_bf")
@@ -53,9 +59,16 @@ def tile_fuzzyclustering_pa_kernel(
         nc.scalar.dma_start(out=alpha_bf[:], in_=sim_alpha.rearrange("(p g) -> p g", g=G))
         nc.scalar.dma_start(out=beta_bf[:], in_=sim_beta.rearrange("(p g) -> p g", g=G))
 
-        def load_clusters(b):
+        def load_clusters(b, first, groups):
             nc.sync.dma_start(
-                out=cl_sb[:, G * b : G * b + G, :], in_=clusters[b].rearrange("(p g) k -> p g k", g=G)
+                out=cl_sb[:, G * b + first : G * b + first + groups, :],
+                in_=clusters[b].rearrange("(p g) k -> p g k", g=G)[:, first : first + groups, :],
+            )
+
+        def load_bias(first, groups):
+            nc.sync.dma_start(
+                out=bias_sb[:, first : first + groups, :],
+                in_=clusters_bias.rearrange("(p g) k -> p g k", g=G)[:, first : first + groups, :],
             )
 
         def load_points(b, half):
@@ -65,11 +78,12 @@ def tile_fuzzyclustering_pa_kernel(
             )
 
         nc.sync.dma_start(out=wc_sb[:], in_=Wc.rearrange("(p g) k -> p g k", g=G))
-        nc.sync.dma_start(out=bias_sb[:], in_=clusters_bias.rearrange("(p g) k -> p g k", g=G))
-        load_clusters(0)
+        for h in range(2):
+            load_bias(2 * h, 2)
+            load_clusters(0, 2 * h, 2)
         load_points(0, 0)
         load_points(0, 1)
-        load_clusters(1)
+        load_clusters(1, 0, G)
         load_points(1, 0)
         load_points(1, 1)
 
@@ -81,6 +95,9 @@ def tile_fuzzyclustering_pa_kernel(
         nc.vector.memset(zero[:], 0.0)
         warm = keep.tile([P, 1], F32, name="warm")
         nc.scalar.activation(out=warm[:], in_=zero[:], func=ACT.Silu)
+
+        def exponential_table():
+            nc.scalar.activation(out=warm[:], in_=zero[:], func=ACT.Exp)
 
         alpha = keep.tile([P, G], F32, name="alpha")
         beta = keep.tile([P, G], F32, name="beta")
@@ -172,24 +189,23 @@ def tile_fuzzyclustering_pa_kernel(
         def centres_regroup(b, h, copy):
             regroup(x_grouped, M * b + PAIR * h, ("x", b, h), copy)
 
-        def centres_in_quantise(b, h):
-            quantise(x_grouped, x_codes, x_scales, M * b + PAIR * h, PAIR)
+        def centres_in_quantise(b):
+            quantise(x_grouped, x_codes, x_scales, M * b, M)
 
-        def centres_matmul(b, h):
-            cols = slice(M * b + PAIR * h, M * b + PAIR * h + PAIR)
+        def centres_matmul(b):
             for t in range(G):
-                z = bank("z", PAIR)
+                z = bank("z")
                 nc.tensor.matmul_mx(
                     out=z[:],
                     lhsT=w_codes[:, P * t : P * t + P].bitcast(FP8X4),
                     lhsT_scale=w_scales[:, P * t : P * t + P],
-                    rhs=x_codes[:, cols].bitcast(FP8X4),
-                    rhs_scale=x_scales[:, cols],
+                    rhs=x_codes[:, M * b : M * b + M].bitcast(FP8X4),
+                    rhs_scale=x_scales[:, M * b : M * b + M],
                     start=True,
                     stop=True,
                 )
                 nc.scalar.activation(
-                    out=c_sb[:, t, cols], in_=z[:], func=ACT.Silu, bias=bc_f[:, t : t + 1], scale=1.0
+                    out=c_sb[:, t, M * b : M * b + M], in_=z[:], func=ACT.Silu, bias=bc_f[:, t : t + 1], scale=1.0
                 )
 
         def centres_turn_back(b, g):
@@ -208,7 +224,7 @@ def tile_fuzzyclustering_pa_kernel(
                 reciprocal_norm(c_rnorm, c_clamped, c_sumsq, col - 1, 2)
 
         def centres_spread(b, h):
-            rn = bank("rn_c", PAIR)
+            rn = factor_bank("rn_c", PAIR)
             for side in range(2):
                 col = G * b + 2 * h + side
                 spread(rn[:, P * side : P * side + P], c_rnorm[:, col : col + 1])
@@ -223,87 +239,87 @@ def tile_fuzzyclustering_pa_kernel(
                 op=ALU.mult,
             )
 
-        def centres_quantise(b, h):
-            quantise(c_grouped, c_codes, c_scales, M * b + PAIR * h, PAIR)
+        def centres_quantise(b):
+            quantise(c_grouped, c_codes, c_scales, M * b, M)
 
-        def points_norm(chunk):
-            reciprocal_norm(p_rnorm, p_clamped, p_sumsq, G * chunk, G)
+        def block_columns(block):
+            b, j = divmod(block, BLOCKS_PER_BATCH)
+            return b, BLOCK * j
 
-        def points_gram(chunk, j):
-            b, half = divmod(chunk, CHUNKS_PER_BATCH)
-            if j == 0:
-                live["gram", chunk] = bank("gram")
-            cols = slice(CHUNK * half + P * j, CHUNK * half + P * j + P)
-            for t in range(G):
-                nc.tensor.matmul(
-                    live["gram", chunk][:, P * j : P * j + P],
-                    lhsT=pts[:, b, t, cols],
-                    rhs=pts[:, b, t, cols],
-                    start=t == 0,
-                    stop=t == G - 1,
+        def points_gram(block):
+            b, first = block_columns(block)
+            gram = bank("gram", BLOCK)
+            for j in range(2):
+                cols = slice(first + P * j, first + P * j + P)
+                for t in range(G):
+                    nc.tensor.matmul(
+                        gram[:, P * j : P * j + P],
+                        lhsT=pts[:, b, t, cols],
+                        rhs=pts[:, b, t, cols],
+                        start=t == 0,
+                        stop=t == G - 1,
+                    )
+            live["gram", block] = gram
+
+        def points_diagonal(block):
+            for j in range(2):
+                col = 2 * block + j
+                nc.vector.scalar_tensor_tensor(
+                    out=diagonal[:],
+                    in0=live["gram", block][:, P * j : P * j + P],
+                    scalar=1.0,
+                    in1=identity[:],
+                    op0=ALU.mult,
+                    op1=ALU.mult,
+                    accum_out=p_sumsq[:, col : col + 1],
                 )
+            reciprocal_norm(p_rnorm, p_clamped, p_sumsq, 2 * block, 2)
 
-        def points_diagonal(chunk, j):
-            nc.vector.scalar_tensor_tensor(
-                out=diagonal[:],
-                in0=live["gram", chunk][:, P * j : P * j + P],
-                scalar=1.0,
-                in1=identity[:],
-                op0=ALU.mult,
-                op1=ALU.mult,
-                accum_out=p_sumsq[:, G * chunk + j : G * chunk + j + 1],
-            )
-            if j == TILES_PER_CHUNK - 1:
-                points_norm(chunk)
-
-        def points_turn(chunk, j):
-            b, half = divmod(chunk, CHUNKS_PER_BATCH)
-            first = CHUNK * half // 2 + P * j
+        def points_turn(block):
+            b, first = block_columns(block)
             f = bank("f")
             for t in range(G):
-                nc.tensor.transpose(f[:, P * t : P * t + P], pts_words[:, b, t, first : first + P], identity[:])
-            live["f", chunk, j] = f
+                nc.tensor.transpose(
+                    f[:, P * t : P * t + P], pts_words[:, b, t, first // 2 : first // 2 + P], identity[:]
+                )
+            live["f", block] = f
 
-        def points_squares(chunk, j):
-            pairs = live["f", chunk, j][:].bitcast(BF16).rearrange("w (d e) -> w e d", e=2)
+        def points_squares(block):
+            pairs = live["f", block][:].bitcast(BF16).rearrange("w (d e) -> w e d", e=2)
             for e in range(2):
-                col = G * chunk + 2 * j + e
+                col = 2 * block + e
                 nc.scalar.activation(
                     out=squares[:], in_=pairs[:, e, :], func=ACT.Square, accum_out=p_sumsq[:, col : col + 1]
                 )
-            if j == 1:
-                points_norm(chunk)
+            reciprocal_norm(p_rnorm, p_clamped, p_sumsq, 2 * block, 2)
 
-        def points_spread(chunk):
-            rn = bank("rn_p")
-            for col in range(G):
-                spread(rn[:, P * col : P * col + P], p_rnorm[:, G * chunk + col : G * chunk + col + 1])
-            live["rn_p", chunk] = rn
+        def points_spread(block):
+            rn = factor_bank("rn_p", BLOCK)
+            for e in range(2):
+                spread(rn[:, P * e : P * e + P], p_rnorm[:, 2 * block + e : 2 * block + e + 1])
+            live["rn_p", block] = rn
 
-        def points_spread_copy(chunk):
-            rn = work.tile([P, CHUNK], F32, name="rn_sb", tag="rn_sb", bufs=2)
-            nc.scalar.copy(out=rn[:], in_=live["rn_p", chunk][:])
-            live["rn_p", chunk] = rn
+        def points_spread_copy(block):
+            rn = work.tile([P, BLOCK], F32, name="rn_sb", tag="rn_sb", bufs=2)
+            nc.scalar.copy(out=rn[:], in_=live["rn_p", block][:])
+            live["rn_p", block] = rn
 
-        def points_scale(chunk, first, width, engine):
-            b, half = divmod(chunk, CHUNKS_PER_BATCH)
-            rn = live["rn_p", chunk]
-            dst = p_grouped[:, CHUNK * chunk + first : CHUNK * chunk + first + width, :]
-            src = pts[:, b, :, CHUNK * half + first : CHUNK * half + first + width]
-            if chunk in GRAM:
+        def points_scale(block, engine):
+            b, first = block_columns(block)
+            rn = live["rn_p", block]
+            dst = p_grouped[:, BLOCK * block : BLOCK * block + BLOCK, :]
+            src = pts[:, b, :, first : first + BLOCK]
+            if block in GRAM:
                 engine.tensor_tensor(
                     out=dst,
-                    in0=rn[:, first : first + width].unsqueeze(2).to_broadcast([P, width, G]),
+                    in0=rn[:].unsqueeze(2).to_broadcast([P, BLOCK, G]),
                     in1=src.rearrange("p t n -> p n t"),
                     op=ALU.mult,
                 )
             else:
-                block, inner = divmod(first, BLOCK)
-                factors = rn[:, BLOCK * block : BLOCK * block + BLOCK].rearrange("p (e w) -> p w e", e=2)
-                factors = factors[:, inner // 2 : (inner + width) // 2, :]
                 engine.tensor_tensor(
                     out=dst.rearrange("p (w e) t -> p w e t", e=2),
-                    in0=factors.unsqueeze(3).to_broadcast([P, width // 2, 2, G]),
+                    in0=rn[:].rearrange("p (e w) -> p w e", e=2).unsqueeze(3).to_broadcast([P, P, 2, G]),
                     in1=src.rearrange("p t (w e) -> p w e t", e=2),
                     op=ALU.mult,
                 )
@@ -387,10 +403,11 @@ def tile_fuzzyclustering_pa_kernel(
         def copy_out(k):
             chunk, quarter = divmod(k, TILES_PER_CHUNK)
             if quarter == 0:
-                live["out", chunk] = work.tile([P, G, CHUNK], F32, name="result", tag="result", bufs=2)
+                live["out", chunk] = work.tile([P, G, CHUNK], F32, name="result", tag="result", bufs=4)
             result = live["out", chunk]
             cols = slice(P * quarter, P * quarter + P)
-            nc.vector.tensor_copy(out=result[:, :, cols], in_=live["o", k][:].rearrange("p (g n) -> p g n", g=G))
+            copy = nc.scalar.copy if k in SCALAR_COPIES else nc.vector.tensor_copy
+            copy(out=result[:, :, cols], in_=live["o", k][:].rearrange("p (g n) -> p g n", g=G))
             b, half = divmod(chunk, CHUNKS_PER_BATCH)
             rows = out[b].rearrange("(p g) n -> p g n", g=G)
             first = CHUNK * half
@@ -402,124 +419,103 @@ def tile_fuzzyclustering_pa_kernel(
         def softmax_step(step):
             if 0 <= step + 1 < TILES:
                 points_onto_partitions(step + 1)
-            if 0 <= step - 6 < TILES:
-                copy_out(step - 6)
             if 0 <= step < TILES:
                 row_max(step)
+            if 0 <= step - 6 < TILES:
+                copy_out(step - 6)
             if 0 <= step - 2 < TILES:
                 normalise(step - 2)
-            chunk, g = divmod(step + 5, G)
-            if 1 <= chunk < CHUNKS:
-                logits(chunk, g)
-            chunk, g = divmod(step + 6, G)
-            if 1 <= chunk < CHUNKS and g % 2 == 0:
+            for chunk, g in SIMILARITIES_IN.get(step, ()):
                 similarities(chunk, g)
-                similarities(chunk, g + 1)
+            for chunk, g in LOGITS_IN.get(step, ()):
+                logits(chunk, g)
             if 0 <= step < TILES:
                 exponentials(step)
             if 0 <= step - 4 < TILES:
                 clusters_onto_partitions(step - 4)
 
         sc, vc = nc.scalar.copy, nc.vector.tensor_copy
-        ve = nc.vector
+        ve, ge = nc.vector, nc.gpsimd
         weights_turn(0)
         weights_turn(1)
         weights_regroup(0, sc)
         weights_regroup(1, sc)
         small_in()
         centres_add(0, 0)
-        centres_add(0, 1)
-        weights_quantise()
         centres_turn(0, 0)
-        centres_turn(0, 1)
-        points_gram(0, 0)
-        points_gram(0, 1)
         centres_regroup(0, 0, sc)
+        centres_add(0, 1)
+        centres_turn(0, 1)
+        weights_quantise()
         centres_regroup(0, 1, sc)
-        points_diagonal(0, 0)
-        points_diagonal(0, 1)
-        centres_in_quantise(0, 0)
-        centres_in_quantise(0, 1)
-        points_turn(1, 0)
-        points_squares(1, 0)
-        points_gram(0, 2)
-        points_gram(0, 3)
-        centres_matmul(0, 0)
-        points_diagonal(0, 2)
-        points_diagonal(0, 3)
+        points_turn(0)
+        points_squares(0)
+        centres_in_quantise(0)
+        points_gram(1)
+        centres_matmul(0)
         centres_add(1, 0)
         centres_add(1, 1)
-        centres_matmul(0, 1)
+        points_diagonal(1)
         centres_turn(1, 0)
         centres_turn(1, 1)
-        centres_regroup(1, 0, vc)
+        centres_regroup(1, 0, sc)
         centres_regroup(1, 1, vc)
+        points_spread(0)
+        points_scale(0, ve)
         centres_turn_back(0, 0)
         centres_turn_back(0, 1)
         centres_squares(0, 0)
         centres_squares(0, 1)
-        points_gram(3, 0)
-        points_gram(3, 1)
+        centres_in_quantise(1)
+        points_spread(1)
+        points_scale(1, ve)
         centres_turn_back(0, 2)
         centres_turn_back(0, 3)
         centres_squares(0, 2)
         centres_squares(0, 3)
-        points_diagonal(3, 0)
-        centres_in_quantise(1, 0)
-        points_diagonal(3, 1)
-        centres_in_quantise(1, 1)
-        points_turn(1, 1)
-        points_squares(1, 1)
-        centres_matmul(1, 0)
-        points_gram(3, 2)
-        points_gram(3, 3)
-        points_spread(0)
-        points_diagonal(3, 2)
-        points_scale(0, 0, 256, ve)
-        points_diagonal(3, 3)
-        points_scale(0, 256, 256, ve)
-        centres_matmul(1, 1)
+        points_gram(2)
+        points_diagonal(2)
+        centres_matmul(1)
+        points_gram(3)
+        points_diagonal(3)
+        points_quantise(0)
         centres_spread(0, 0)
         centres_scale(0, 0)
-        points_quantise(0)
-        points_turn(2, 0)
+        points_turn(5)
+        points_squares(5)
         centres_spread(0, 1)
         centres_scale(0, 1)
-        centres_quantise(0, 0)
-        points_squares(2, 0)
         centres_turn_back(1, 0)
         centres_turn_back(1, 1)
         centres_squares(1, 0)
         centres_squares(1, 1)
-        points_spread(1)
-        points_scale(1, 0, 256, ve)
-        centres_quantise(0, 1)
+        points_spread(2)
+        points_gram(4)
+        points_diagonal(4)
+        points_spread(3)
+        centres_quantise(0)
+        points_scale(2, ve)
+        exponential_table()
+        for g in range(G):
+            similarities(0, g)
+        for g in range(G):
+            logits(0, g)
+        centres_spread(1, 0)
+        points_scale(3, ve)
+        points_quantise(1)
+        centres_scale(1, 0)
         centres_turn_back(1, 2)
         centres_turn_back(1, 3)
         centres_squares(1, 2)
         centres_squares(1, 3)
-        points_turn(2, 1)
-        points_spread(3)
-        points_squares(2, 1)
-        points_spread_copy(3)
-        for first in range(0, 512, 128):
-            points_scale(3, first, 128, nc.gpsimd)
-        for g in range(G):
-            similarities(0, g)
-        points_scale(1, 256, 256, ve)
-        for g in range(G):
-            logits(0, g)
-        points_quantise(1)
-        centres_spread(1, 0)
-        centres_scale(1, 0)
-        centres_spread(1, 1)
-        centres_scale(1, 1)
-        centres_quantise(1, 0)
-        centres_quantise(1, 1)
+        points_turn(6)
         between = {
-            -1: lambda: (points_spread(2), points_scale(2, 0, 256, ve)),
-            0: lambda: points_scale(2, 256, 256, ve),
-            1: lambda: points_quantise(2),
+            -1: lambda: points_squares(6),
+            0: lambda: (points_spread(4), points_scale(4, ve)),
+            1: lambda: (centres_spread(1, 1), centres_scale(1, 1), points_turn(7)),
+            2: lambda: (points_spread(5), points_scale(5, ve), centres_quantise(1), points_squares(7)),
+            3: lambda: (points_spread(6), points_quantise(2), points_scale(6, ve)),
+            4: lambda: (points_spread(7), points_scale(7, ve)),
             5: lambda: points_quantise(3),
         }
         for step in range(-2, TILES + 6):

@@ -25,6 +25,7 @@ GRAM = (1, 2, 3, 4)
 SIMILARITIES_IN = {-2: ((1, 0), (1, 1)), 1: ((1, 2), (1, 3)), 4: ((2, 0), (2, 1)), 5: ((2, 2), (2, 3)), 7: ((3, 0), (3, 1)), 9: ((3, 2), (3, 3))}
 LOGITS_IN = {0: ((1, 0),), 1: ((1, 1),), 2: ((1, 2),(1, 3)), 5: ((2, 0), (2, 1)), 6: ((2, 2), (2, 3)), 8: ((3, 0),), 9: ((3, 1),), 10: ((3, 2), (3, 3))}
 SCALAR_COPIES = (5, 7, 9, 11, 13, 15)
+RUN = 4
 TILES = B * N // P
 TILES_PER_CHUNK = CHUNK // P
 PAIR = 2 * P
@@ -233,9 +234,12 @@ def tile_fuzzyclustering_pa_kernel(
         def centres_scale(b, h):
             cols = slice(M * b + PAIR * h, M * b + PAIR * h + PAIR)
             nc.vector.tensor_tensor(
-                out=c_grouped[:, cols, :],
-                in0=live["rn_c", b, h][:].unsqueeze(2).to_broadcast([P, PAIR, G]),
-                in1=c_sb[:, :, cols].rearrange("p t m -> p m t"),
+                out=c_grouped[:, cols, :].rearrange("p (c i) t -> p c t i", i=RUN),
+                in0=live["rn_c", b, h][:]
+                .rearrange("p (c i) -> p c i", i=RUN)
+                .unsqueeze(2)
+                .to_broadcast([P, PAIR // RUN, G, RUN]),
+                in1=c_sb[:, :, cols].rearrange("p t (c i) -> p c t i", i=RUN),
                 op=ALU.mult,
             )
 
@@ -311,16 +315,16 @@ def tile_fuzzyclustering_pa_kernel(
             src = pts[:, b, :, first : first + BLOCK]
             if block in GRAM:
                 engine.tensor_tensor(
-                    out=dst,
-                    in0=rn[:].unsqueeze(2).to_broadcast([P, BLOCK, G]),
-                    in1=src.rearrange("p t n -> p n t"),
+                    out=dst.rearrange("p (c i) t -> p c t i", i=RUN),
+                    in0=rn[:].rearrange("p (c i) -> p c i", i=RUN).unsqueeze(2).to_broadcast([P, BLOCK // RUN, G, RUN]),
+                    in1=src.rearrange("p t (c i) -> p c t i", i=RUN),
                     op=ALU.mult,
                 )
             else:
                 engine.tensor_tensor(
-                    out=dst.rearrange("p (w e) t -> p w e t", e=2),
-                    in0=rn[:].rearrange("p (e w) -> p w e", e=2).unsqueeze(3).to_broadcast([P, P, 2, G]),
-                    in1=src.rearrange("p t (w e) -> p w e t", e=2),
+                    out=dst.rearrange("p (w e) t -> p w t e", e=2),
+                    in0=rn[:].rearrange("p (e w) -> p w e", e=2).unsqueeze(2).to_broadcast([P, P, G, 2]),
+                    in1=src.rearrange("p t (w e) -> p w t e", e=2),
                     op=ALU.mult,
                 )
 

@@ -415,8 +415,12 @@ def tile_fuzzyclustering_pa_kernel(
             b, half = divmod(chunk, CHUNKS_PER_BATCH)
             rows = out[b].rearrange("(p g) n -> p g n", g=G)
             first = CHUNK * half
-            if chunk == CHUNKS - 1:
+            if k >= 14:
                 nc.sync.dma_start(out=rows[:, :, first + P * quarter : first + P * quarter + P], in_=result[:, :, cols])
+            elif k >= 0:
+                if quarter % 2 == 1:
+                    two = slice(first + P * quarter - P, first + P * quarter + P)
+                    nc.sync.dma_start(out=rows[:, :, two], in_=result[:, :, P * quarter - P : P * quarter + P])
             elif quarter == TILES_PER_CHUNK - 1:
                 nc.sync.dma_start(out=rows[:, :, first : first + CHUNK], in_=result[:])
 

@@ -221,8 +221,9 @@ def tile_fuzzyclustering_pa_kernel(
             nc.scalar.activation(
                 out=squares[:], in_=live["ct", b, g][:], func=ACT.Square, accum_out=c_sumsq[:, col : col + 1]
             )
-            if g % 2 == 1:
-                reciprocal_norm(c_rnorm, c_clamped, c_sumsq, col - 1, 2)
+
+        def centres_norm(b, first, groups):
+            reciprocal_norm(c_rnorm, c_clamped, c_sumsq, G * b + first, groups)
 
         def centres_spread(b, h):
             rn = factor_bank("rn_c", PAIR)
@@ -277,7 +278,6 @@ def tile_fuzzyclustering_pa_kernel(
                     op1=ALU.mult,
                     accum_out=p_sumsq[:, col : col + 1],
                 )
-            reciprocal_norm(p_rnorm, p_clamped, p_sumsq, 2 * block, 2)
 
         def points_turn(block):
             b, first = block_columns(block)
@@ -295,7 +295,9 @@ def tile_fuzzyclustering_pa_kernel(
                 nc.scalar.activation(
                     out=squares[:], in_=pairs[:, e, :], func=ACT.Square, accum_out=p_sumsq[:, col : col + 1]
                 )
-            reciprocal_norm(p_rnorm, p_clamped, p_sumsq, 2 * block, 2)
+
+        def points_norm(block, blocks):
+            reciprocal_norm(p_rnorm, p_clamped, p_sumsq, 2 * block, 2 * blocks)
 
         def points_spread(block):
             rn = factor_bank("rn_p", BLOCK)
@@ -458,12 +460,14 @@ def tile_fuzzyclustering_pa_kernel(
         centres_regroup(0, 1, sc)
         points_turn(0)
         points_squares(0)
+        points_norm(0, 1)
         centres_in_quantise(0)
         points_gram(1)
         centres_matmul(0)
         centres_add(1, 0)
         centres_add(1, 1)
         points_diagonal(1)
+        points_norm(1, 1)
         centres_turn(1, 0)
         centres_turn(1, 1)
         centres_regroup(1, 0, sc)
@@ -474,6 +478,7 @@ def tile_fuzzyclustering_pa_kernel(
         centres_turn_back(0, 1)
         centres_squares(0, 0)
         centres_squares(0, 1)
+        centres_norm(0, 0, 2)
         centres_in_quantise(1)
         points_spread(1)
         points_scale(1, ve)
@@ -481,11 +486,13 @@ def tile_fuzzyclustering_pa_kernel(
         centres_turn_back(0, 3)
         centres_squares(0, 2)
         centres_squares(0, 3)
+        centres_norm(0, 2, 2)
         points_gram(2)
         points_diagonal(2)
         centres_matmul(1)
         points_gram(3)
         points_diagonal(3)
+        points_norm(2, 2)
         points_quantise(0)
         centres_spread(0, 0)
         centres_scale(0, 0)
@@ -497,9 +504,11 @@ def tile_fuzzyclustering_pa_kernel(
         centres_turn_back(1, 1)
         centres_squares(1, 0)
         centres_squares(1, 1)
-        points_spread(2)
+        centres_norm(1, 0, 2)
         points_gram(4)
         points_diagonal(4)
+        points_norm(4, 2)
+        points_spread(2)
         points_spread(3)
         centres_quantise(0)
         points_scale(2, ve)
@@ -516,12 +525,13 @@ def tile_fuzzyclustering_pa_kernel(
         centres_turn_back(1, 3)
         centres_squares(1, 2)
         centres_squares(1, 3)
+        centres_norm(1, 2, 2)
         points_turn(6)
         between = {
-            -1: lambda: points_squares(6),
+            -1: lambda: (points_squares(6), points_norm(6, 1)),
             0: lambda: (points_spread(4), points_scale(4, ve)),
             1: lambda: (centres_spread(1, 1), centres_scale(1, 1), points_turn(7)),
-            2: lambda: (points_spread(5), points_scale(5, ve), centres_quantise(1), points_squares(7)),
+            2: lambda: (points_spread(5), points_scale(5, ve), centres_quantise(1), points_squares(7), points_norm(7, 1)),
             3: lambda: (points_spread(6), points_quantise(2), points_scale(6, ve)),
             4: lambda: (points_spread(7), points_scale(7, ve)),
             5: lambda: points_quantise(3),

@@ -55,7 +55,7 @@ def tile_fuzzyclustering_pa_kernel(
         bias_sb = keep.tile([P, G, D], BF16, name="bias_sb")
         cl_sb = keep.tile([P, B * G, D], BF16, name="cl_sb")
         wc_sb = keep.tile([P, G, D], BF16, name="wc_sb")
-        pts = keep.tile([P, B, G, N], BF16, name="pts")
+        pts = [keep.tile([P, G, CHUNK], BF16, name="pts" + str(chunk)) for chunk in range(CHUNKS)]
         nc.scalar.dma_start(out=bc_bf[:], in_=bc.rearrange("(p g) -> p g", g=G))
         nc.scalar.dma_start(out=alpha_bf[:], in_=sim_alpha.rearrange("(p g) -> p g", g=G))
         nc.scalar.dma_start(out=beta_bf[:], in_=sim_beta.rearrange("(p g) -> p g", g=G))
@@ -75,7 +75,7 @@ def tile_fuzzyclustering_pa_kernel(
         def load_points(b, half):
             cols = slice(CHUNK * half, CHUNK * half + CHUNK)
             nc.sync.dma_start(
-                out=pts[:, b, :, cols], in_=points[b].rearrange("(p t) n -> p t n", t=G)[:, :, cols]
+                out=pts[CHUNKS_PER_BATCH * b + half][:], in_=points[b].rearrange("(p t) n -> p t n", t=G)[:, :, cols]
             )
 
         nc.sync.dma_start(out=wc_sb[:], in_=Wc.rearrange("(p g) k -> p g k", g=G))
@@ -83,8 +83,8 @@ def tile_fuzzyclustering_pa_kernel(
             load_bias(2 * h, 2)
             load_clusters(0, 2 * h, 2)
         load_points(0, 0)
-        load_points(0, 1)
         load_clusters(1, 0, G)
+        load_points(0, 1)
         load_points(1, 0)
         load_points(1, 1)
 
@@ -116,7 +116,7 @@ def tile_fuzzyclustering_pa_kernel(
         c_scales = keep.tile([P, B * M], U8, name="c_scales", align_bytes=64)
         p_codes = keep.tile([P, B * N], U32, name="p_codes", align_bytes=64)
         p_scales = keep.tile([P, B * N], U8, name="p_scales", align_bytes=64)
-        c_sb = keep.tile([P, G, B * M], F32, name="c_sb")
+        c_sb = [keep.tile([P, G, M], F32, name="c_sb" + str(b)) for b in range(B)]
         diagonal = keep.tile([P, P], BF16, name="diagonal")
         squares = keep.tile([P, CHUNK], BF16, name="squares")
         c_sumsq = keep.tile([P, B * G], F32, name="c_sumsq")
@@ -125,7 +125,6 @@ def tile_fuzzyclustering_pa_kernel(
         p_sumsq = keep.tile([P, 2 * BLOCKS], F32, name="p_sumsq")
         p_clamped = keep.tile([P, 2 * BLOCKS], F32, name="p_clamped")
         p_rnorm = keep.tile([P, 2 * BLOCKS], F32, name="p_rnorm")
-        pts_words = pts[:].bitcast(F32)
         live = {}
 
         def quantise(grouped, codes, scales, first, cols):
@@ -206,14 +205,14 @@ def tile_fuzzyclustering_pa_kernel(
                     stop=True,
                 )
                 nc.scalar.activation(
-                    out=c_sb[:, t, M * b : M * b + M], in_=z[:], func=ACT.Silu, bias=bc_f[:, t : t + 1], scale=1.0
+                    out=c_sb[b][:, t, :], in_=z[:], func=ACT.Silu, bias=bc_f[:, t : t + 1], scale=1.0
                 )
 
         def centres_turn_back(b, g):
-            first = M * b + P * g
+            first = P * g
             ct = bank("ct")
             for t in range(G):
-                nc.tensor.transpose(ct[:, P * t : P * t + P], c_sb[:, t, first : first + P], identity[:])
+                nc.tensor.transpose(ct[:, P * t : P * t + P], c_sb[b][:, t, first : first + P], identity[:])
             live["ct", b, g] = ct
 
         def centres_squares(b, g):
@@ -240,7 +239,7 @@ def tile_fuzzyclustering_pa_kernel(
                 .rearrange("p (c i) -> p c i", i=RUN)
                 .unsqueeze(2)
                 .to_broadcast([P, PAIR // RUN, G, RUN]),
-                in1=c_sb[:, :, cols].rearrange("p t (c i) -> p c t i", i=RUN),
+                in1=c_sb[b][:, :, PAIR * h : PAIR * h + PAIR].rearrange("p t (c i) -> p c t i", i=RUN),
                 op=ALU.mult,
             )
 
@@ -248,19 +247,19 @@ def tile_fuzzyclustering_pa_kernel(
             quantise(c_grouped, c_codes, c_scales, M * b, M)
 
         def block_columns(block):
-            b, j = divmod(block, BLOCKS_PER_BATCH)
-            return b, BLOCK * j
+            chunk, j = divmod(block, 2)
+            return chunk, BLOCK * j
 
         def points_gram(block):
-            b, first = block_columns(block)
+            chunk, first = block_columns(block)
             gram = bank("gram", BLOCK)
             for j in range(2):
                 cols = slice(first + P * j, first + P * j + P)
                 for t in range(G):
                     nc.tensor.matmul(
                         gram[:, P * j : P * j + P],
-                        lhsT=pts[:, b, t, cols],
-                        rhs=pts[:, b, t, cols],
+                        lhsT=pts[chunk][:, t, cols],
+                        rhs=pts[chunk][:, t, cols],
                         start=t == 0,
                         stop=t == G - 1,
                     )
@@ -280,11 +279,12 @@ def tile_fuzzyclustering_pa_kernel(
                 )
 
         def points_turn(block):
-            b, first = block_columns(block)
+            chunk, first = block_columns(block)
             f = bank("f")
+            words = pts[chunk][:].bitcast(F32)
             for t in range(G):
                 nc.tensor.transpose(
-                    f[:, P * t : P * t + P], pts_words[:, b, t, first // 2 : first // 2 + P], identity[:]
+                    f[:, P * t : P * t + P], words[:, t, first // 2 : first // 2 + P], identity[:]
                 )
             live["f", block] = f
 
@@ -310,22 +310,26 @@ def tile_fuzzyclustering_pa_kernel(
             nc.scalar.copy(out=rn[:], in_=live["rn_p", block][:])
             live["rn_p", block] = rn
 
-        def points_scale(block, engine):
-            b, first = block_columns(block)
+        def points_scale(block, engine, skip=0, width=BLOCK):
+            chunk, first = block_columns(block)
             rn = live["rn_p", block]
-            dst = p_grouped[:, BLOCK * block : BLOCK * block + BLOCK, :]
-            src = pts[:, b, :, first : first + BLOCK]
+            dst = p_grouped[:, BLOCK * block + skip : BLOCK * block + skip + width, :]
+            src = pts[chunk][:, :, first + skip : first + skip + width]
             if block in GRAM:
                 engine.tensor_tensor(
                     out=dst.rearrange("p (c i) t -> p c t i", i=RUN),
-                    in0=rn[:].rearrange("p (c i) -> p c i", i=RUN).unsqueeze(2).to_broadcast([P, BLOCK // RUN, G, RUN]),
+                    in0=rn[:, skip : skip + width]
+                    .rearrange("p (c i) -> p c i", i=RUN)
+                    .unsqueeze(2)
+                    .to_broadcast([P, width // RUN, G, RUN]),
                     in1=src.rearrange("p t (c i) -> p c t i", i=RUN),
                     op=ALU.mult,
                 )
             else:
+                pairs = rn[:].rearrange("p (e w) -> p w e", e=2)[:, skip // 2 : (skip + width) // 2, :]
                 engine.tensor_tensor(
                     out=dst.rearrange("p (w e) t -> p w t e", e=2),
-                    in0=rn[:].rearrange("p (e w) -> p w e", e=2).unsqueeze(2).to_broadcast([P, P, G, 2]),
+                    in0=pairs.unsqueeze(2).to_broadcast([P, width // 2, G, 2]),
                     in1=src.rearrange("p t (w e) -> p w t e", e=2),
                     op=ALU.mult,
                 )
@@ -407,24 +411,22 @@ def tile_fuzzyclustering_pa_kernel(
             live["o", k] = o
 
         def copy_out(k):
-            chunk, quarter = divmod(k, TILES_PER_CHUNK)
-            if quarter == 0:
-                live["out", chunk] = work.tile([P, G, CHUNK], F32, name="result", tag="result", bufs=4)
-            result = live["out", chunk]
-            cols = slice(P * quarter, P * quarter + P)
+            together = 2 if k < TILES - 2 else 1
+            place = k % together
+            if place == 0:
+                live["out"] = work.tile([P, G, P * together], F32, name="result", tag="result" + str(together), bufs=7)
+            result = live["out"]
             copy = nc.scalar.copy if k in SCALAR_COPIES else nc.vector.tensor_copy
-            copy(out=result[:, :, cols], in_=live["o", k][:].rearrange("p (g n) -> p g n", g=G))
-            b, half = divmod(chunk, CHUNKS_PER_BATCH)
-            rows = out[b].rearrange("(p g) n -> p g n", g=G)
-            first = CHUNK * half
-            if k >= 14:
-                nc.sync.dma_start(out=rows[:, :, first + P * quarter : first + P * quarter + P], in_=result[:, :, cols])
-            elif k >= 0:
-                if quarter % 2 == 1:
-                    two = slice(first + P * quarter - P, first + P * quarter + P)
-                    nc.sync.dma_start(out=rows[:, :, two], in_=result[:, :, P * quarter - P : P * quarter + P])
-            elif quarter == TILES_PER_CHUNK - 1:
-                nc.sync.dma_start(out=rows[:, :, first : first + CHUNK], in_=result[:])
+            copy(
+                out=result[:, :, P * place : P * place + P],
+                in_=live["o", k][:].rearrange("p (g n) -> p g n", g=G),
+            )
+            if place == together - 1:
+                b, quarter = divmod(k + 1 - together, N // P)
+                first = P * quarter
+                nc.sync.dma_start(
+                    out=out[b].rearrange("(p g) n -> p g n", g=G)[:, :, first : first + P * together], in_=result[:]
+                )
 
         def softmax_step(step):
             if 0 <= step + 1 < TILES:
@@ -468,12 +470,12 @@ def tile_fuzzyclustering_pa_kernel(
         centres_add(1, 1)
         points_diagonal(1)
         points_norm(1, 1)
+        points_spread(0)
         centres_turn(1, 0)
         centres_turn(1, 1)
+        points_scale(0, ve)
         centres_regroup(1, 0, sc)
         centres_regroup(1, 1, vc)
-        points_spread(0)
-        points_scale(0, ve)
         centres_turn_back(0, 0)
         centres_turn_back(0, 1)
         centres_squares(0, 0)
@@ -528,13 +530,13 @@ def tile_fuzzyclustering_pa_kernel(
         centres_norm(1, 2, 2)
         points_turn(6)
         between = {
-            -1: lambda: (points_squares(6), points_norm(6, 1)),
-            0: lambda: (points_spread(4), points_scale(4, ve)),
-            1: lambda: (centres_spread(1, 1), centres_scale(1, 1), points_turn(7)),
-            2: lambda: (points_spread(5), points_scale(5, ve), centres_quantise(1), points_squares(7), points_norm(7, 1)),
-            3: lambda: (points_spread(6), points_quantise(2), points_scale(6, ve)),
-            4: lambda: (points_spread(7), points_scale(7, ve)),
-            5: lambda: points_quantise(3),
+            -1: lambda: (points_squares(6), points_norm(6, 1),),
+            0: lambda: (points_spread(4), points_scale(4, ve),),
+            1: lambda: (points_spread(5), points_scale(5, ve), centres_spread(1, 1), points_turn(7),),
+            2: lambda: (centres_scale(1, 1), points_quantise(2), centres_quantise(1), points_squares(7), points_norm(7, 1),),
+            3: lambda: (points_spread(6), points_scale(6, ve),),
+            4: lambda: (points_spread(7), points_scale(7, ve),),
+            5: lambda: (points_quantise(3),),
         }
         for step in range(-2, TILES + 6):
             softmax_step(step)

@@ -21,7 +21,7 @@ CHUNKS = B * CHUNKS_PER_BATCH
 BLOCK = 256
 BLOCKS_PER_BATCH = N // BLOCK
 BLOCKS = B * BLOCKS_PER_BATCH
-GRAM = (1, 2, 3, 4)
+GRAM = (1, 2, 3, 4, 6)
 SIMILARITIES_IN = {-2: ((1, 0), (1, 1)), 1: ((1, 2), (1, 3)), 4: ((2, 0), (2, 1)), 5: ((2, 2), (2, 3)), 7: ((3, 0), (3, 1)), 9: ((3, 2), (3, 3))}
 LOGITS_IN = {0: ((1, 0),), 1: ((1, 1),), 2: ((1, 2),(1, 3)), 5: ((2, 0), (2, 1)), 6: ((2, 2), (2, 3)), 8: ((3, 0),), 9: ((3, 1),), 10: ((3, 2), (3, 3))}
 SCALAR_COPIES = (5, 7, 9, 11, 13, 15)
@@ -92,6 +92,8 @@ def tile_fuzzyclustering_pa_kernel(
         make_identity(nc, identity[:])
         minus_half = keep.tile([P, G], F32, name="minus_half")
         nc.vector.memset(minus_half[:], -0.5)
+        ones = keep.tile([P, 1], F32, name="ones")
+        nc.vector.memset(ones[:], 1.0)
         zero = keep.tile([P, 1], F32, name="zero")
         nc.vector.memset(zero[:], 0.0)
         warm = keep.tile([P, 1], F32, name="warm")
@@ -296,6 +298,35 @@ def tile_fuzzyclustering_pa_kernel(
                     out=squares[:], in_=pairs[:, e, :], func=ACT.Square, accum_out=p_sumsq[:, col : col + 1]
                 )
 
+        def points_square(block):
+            chunk, first = block_columns(block)
+            src = pts[chunk][:, :, first : first + BLOCK]
+            sq = work.tile([P, G, BLOCK], F32, name="sq", tag="sq", bufs=2)
+            nc.gpsimd.tensor_tensor(out=sq[:], in0=src, in1=src, op=ALU.mult)
+            live["sq", block] = sq
+
+        def points_sums(block):
+            sums = bank("sums", 2)
+            for j in range(2):
+                for t in range(G):
+                    nc.tensor.matmul(
+                        sums[:, j : j + 1],
+                        lhsT=live["sq", block][:, t, P * j : P * j + P],
+                        rhs=ones[:],
+                        start=t == 0,
+                        stop=t == G - 1,
+                    )
+            live["sums", block] = sums
+
+        def points_sums_norm(block):
+            clamped = work.tile([P, 2], F32, name="clamped", tag="clamped", bufs=2)
+            nc.vector.tensor_scalar(
+                out=clamped[:], in0=live["sums", block][:], scalar1=NORM_EPS_SQUARED, scalar2=None, op0=ALU.max
+            )
+            nc.gpsimd.tensor_tensor(
+                out=p_rnorm[:, 2 * block : 2 * block + 2], in0=clamped[:], in1=minus_half[:, 0:2], op=ALU.pow
+            )
+
         def points_norm(block, blocks):
             reciprocal_norm(p_rnorm, p_clamped, p_sumsq, 2 * block, 2 * blocks)
 
@@ -470,6 +501,7 @@ def tile_fuzzyclustering_pa_kernel(
         centres_add(1, 1)
         points_diagonal(1)
         points_norm(1, 1)
+        points_square(6)
         points_spread(0)
         centres_turn(1, 0)
         centres_turn(1, 1)
@@ -514,6 +546,8 @@ def tile_fuzzyclustering_pa_kernel(
         points_spread(3)
         centres_quantise(0)
         points_scale(2, ve)
+        points_sums(6)
+        points_sums_norm(6)
         exponential_table()
         for g in range(G):
             similarities(0, g)
@@ -528,14 +562,17 @@ def tile_fuzzyclustering_pa_kernel(
         centres_squares(1, 2)
         centres_squares(1, 3)
         centres_norm(1, 2, 2)
-        points_turn(6)
+        points_turn(7)
+        points_spread(5)
+        points_spread_copy(5)
+        points_scale(5, ge)
         between = {
-            -1: lambda: (points_squares(6), points_norm(6, 1),),
+            -1: lambda: (points_squares(7), points_norm(7, 1),),
             0: lambda: (points_spread(4), points_scale(4, ve),),
-            1: lambda: (points_spread(5), points_scale(5, ve), centres_spread(1, 1), points_turn(7),),
-            2: lambda: (centres_scale(1, 1), points_quantise(2), centres_quantise(1), points_squares(7), points_norm(7, 1),),
-            3: lambda: (points_spread(6), points_scale(6, ve),),
-            4: lambda: (points_spread(7), points_scale(7, ve),),
+            1: lambda: (centres_spread(1, 1), centres_scale(1, 1),),
+            2: lambda: (points_quantise(2), centres_quantise(1),),
+            3: lambda: (points_spread(6), points_scale(6, ve), points_spread(7),),
+            4: lambda: (points_scale(7, ve),),
             5: lambda: (points_quantise(3),),
         }
         for step in range(-2, TILES + 6):

from contextlib import ExitStack

import concourse.mybir as mybir
from concourse.masks import make_identity

F32 = mybir.dt.float32
BF16 = mybir.dt.bfloat16
U32 = mybir.dt.uint32
U8 = mybir.dt.uint8
FP8X4 = mybir.dt.float8_e4m3fn_x4
ACT = mybir.ActivationFunctionType
ALU = mybir.AluOpType
AX = mybir.AxisListType

P = 128
G = 4
B, M, D, N = 2, 512, 512, 1024
CHUNK = 512
CHUNKS_PER_BATCH = N // CHUNK
CHUNKS = B * CHUNKS_PER_BATCH
BLOCK = 256
BLOCKS_PER_BATCH = N // BLOCK
BLOCKS = B * BLOCKS_PER_BATCH
GRAM = (1, 2, 3, 4, 6)
SIMILARITIES_IN = {-2: ((1, 0), (1, 1)), 1: ((1, 2), (1, 3)), 4: ((2, 0), (2, 1)), 5: ((2, 2), (2, 3)), 7: ((3, 0), (3, 1)), 9: ((3, 2), (3, 3))}
LOGITS_IN = {0: ((1, 0),), 1: ((1, 1),), 2: ((1, 2),(1, 3)), 5: ((2, 0), (2, 1)), 6: ((2, 2), (2, 3)), 8: ((3, 0),), 9: ((3, 1),), 10: ((3, 2), (3, 3))}
SCALAR_COPIES = (5, 7, 9, 11, 13, 15)
RUN = 4
TILES = B * N // P
TILES_PER_CHUNK = CHUNK // P
PAIR = 2 * P
FLOPS = 2 * B * M * D * D + 2 * B * M * D * N
NORM_EPS_SQUARED = 1e-24


def tile_fuzzyclustering_pa_kernel(
    tc, points, clusters, sim_alpha, sim_beta, clusters_bias, Wc, bc, out
):
    nc = tc.nc
    with ExitStack() as ctx:
        keep = ctx.enter_context(tc.tile_pool(name="keep", bufs=1))
        work = ctx.enter_context(tc.tile_pool(name="work", bufs=2))
        psum = ctx.enter_context(tc.psum_pool(name="psum", bufs=8))
        ctx.enter_context(tc.manual_schedule())

        def bank(name, width=CHUNK):
            return psum.tile([P, width], F32, tag="bank", name=name)

        def factor_bank(name, width):
            return psum.tile([P, width], F32, tag="bank", name=name)

        alpha_bf = keep.tile([P, G], BF16, name="alpha_bf")
        beta_bf = keep.tile([P, G], BF16, name="beta_bf")
        bc_bf = keep.tile([P, G], BF16, name="bc_bf")
        bias_sb = keep.tile([P, G, D], BF16, name="bias_sb")
        cl_sb = keep.tile([P, B * G, D], BF16, name="cl_sb")
        wc_sb = keep.tile([P, G, D], BF16, name="wc_sb")
        pts = [keep.tile([P, G, CHUNK], BF16, name="pts" + str(chunk)) for chunk in range(CHUNKS)]
        nc.scalar.dma_start(out=bc_bf[:], in_=bc.rearrange("(p g) -> p g", g=G))
        nc.scalar.dma_start(out=alpha_bf[:], in_=sim_alpha.rearrange("(p g) -> p g", g=G))
        nc.scalar.dma_start(out=beta_bf[:], in_=sim_beta.rearrange("(p g) -> p g", g=G))

        def load_clusters(b, first, groups):
            nc.sync.dma_start(
                out=cl_sb[:, G * b + first : G * b + first + groups, :],
                in_=clusters[b].rearrange("(p g) k -> p g k", g=G)[:, first : first + groups, :],
            )

        def load_bias(first, groups):
            nc.sync.dma_start(
                out=bias_sb[:, first : first + groups, :],
                in_=clusters_bias.rearrange("(p g) k -> p g k", g=G)[:, first : first + groups, :],
            )

        def load_points(b, half):
            cols = slice(CHUNK * half, CHUNK * half + CHUNK)
            nc.sync.dma_start(
                out=pts[CHUNKS_PER_BATCH * b + half][:], in_=points[b].rearrange("(p t) n -> p t n", t=G)[:, :, cols]
            )

        nc.sync.dma_start(out=wc_sb[:], in_=Wc.rearrange("(p g) k -> p g k", g=G))
        for h in range(2):
            load_bias(2 * h, 2)
            load_clusters(0, 2 * h, 2)
        load_points(0, 0)
        load_clusters(1, 0, G)
        load_points(0, 1)
        load_points(1, 0)
        load_points(1, 1)

        identity = keep.tile([P, P], F32, name="identity")
        make_identity(nc, identity[:])
        minus_half = keep.tile([P, G], F32, name="minus_half")
        nc.vector.memset(minus_half[:], -0.5)
        ones = keep.tile([P, 1], F32, name="ones")
        nc.vector.memset(ones[:], 1.0)
        zero = keep.tile([P, 1], F32, name="zero")
        nc.vector.memset(zero[:], 0.0)
        warm = keep.tile([P, 1], F32, name="warm")
        nc.scalar.activation(out=warm[:], in_=zero[:], func=ACT.Silu)

        def exponential_table():
            nc.scalar.activation(out=warm[:], in_=zero[:], func=ACT.Exp)

        alpha = keep.tile([P, G], F32, name="alpha")
        beta = keep.tile([P, G], F32, name="beta")
        bc_f = keep.tile([P, G], F32, name="bc_f")
        x_rows = keep.tile([P, B * G, D], BF16, name="x_rows")
        w_grouped = keep.tile([P, D, G], BF16, name="w_grouped", align_bytes=64)
        x_grouped = keep.tile([P, B * M, G], BF16, name="x_grouped", align_bytes=64)
        c_grouped = keep.tile([P, B * M, G], BF16, name="c_grouped", align_bytes=64)
        p_grouped = keep.tile([P, B * N, G], BF16, name="p_grouped", align_bytes=64)
        w_codes = keep.tile([P, D], U32, name="w_codes", align_bytes=64)
        w_scales = keep.tile([P, D], U8, name="w_scales", align_bytes=64)
        x_codes = keep.tile([P, B * M], U32, name="x_codes", align_bytes=64)
        x_scales = keep.tile([P, B * M], U8, name="x_scales", align_bytes=64)
        c_codes = keep.tile([P, B * M], U32, name="c_codes", align_bytes=64)
        c_scales = keep.tile([P, B * M], U8, name="c_scales", align_bytes=64)
        p_codes = keep.tile([P, B * N], U32, name="p_codes", align_bytes=64)
        p_scales = keep.tile([P, B * N], U8, name="p_scales", align_bytes=64)
        c_sb = [keep.tile([P, G, M], F32, name="c_sb" + str(b)) for b in range(B)]
        diagonal = keep.tile([P, P], BF16, name="diagonal")
        squares = keep.tile([P, CHUNK], BF16, name="squares")
        c_sumsq = keep.tile([P, B * G], F32, name="c_sumsq")
        c_clamped = keep.tile([P, B * G], F32, name="c_clamped")
        c_rnorm = keep.tile([P, B * G], F32, name="c_rnorm")
        p_sumsq = keep.tile([P, 2 * BLOCKS], F32, name="p_sumsq")
        p_clamped = keep.tile([P, 2 * BLOCKS], F32, name="p_clamped")
        p_rnorm = keep.tile([P, 2 * BLOCKS], F32, name="p_rnorm")
        live = {}

        def quantise(grouped, codes, scales, first, cols):
            nc.vector.quantize_mx(
                out=codes[:, first : first + cols].bitcast(FP8X4),
                scales=scales[:, first : first + cols],
                in_=grouped[:, first : first + cols, :].rearrange("p c t -> p (c t)"),
            )

        def reciprocal_norm(rnorm, clamped, sumsq, first, width):
            cols = slice(first, first + width)
            nc.gpsimd.tensor_scalar(
                out=clamped[:, cols], in0=sumsq[:, cols], scalar1=NORM_EPS_SQUARED, scalar2=None, op0=ALU.max
            )
            nc.gpsimd.tensor_tensor(
                out=rnorm[:, cols], in0=clamped[:, cols], in1=minus_half[:, 0:width], op=ALU.pow
            )

        def spread(dst, column):
            nc.tensor.transpose(dst, column.to_broadcast([P, P]), identity[:])

        def words_onto_partitions(src, first):
            kt = bank("kt")
            words = src[:].bitcast(F32)
            for side in range(2):
                for u in range(2):
                    col = PAIR * u + P * side
                    nc.tensor.transpose(
                        kt[:, col : col + P], words[:, first + side, P * u : P * u + P], identity[:]
                    )
            return kt

        def regroup(dst, offset, key, copy):
            copy(
                out=dst[:].bitcast(F32)[:, offset : offset + PAIR, :],
                in_=live[key][:].rearrange("q (u c) -> q c u", u=2),
            )

        def weights_turn(h):
            live["w", h] = words_onto_partitions(wc_sb, 2 * h)

        def weights_regroup(h, copy):
            regroup(w_grouped, PAIR * h, ("w", h), copy)

        def weights_quantise():
            quantise(w_grouped, w_codes, w_scales, 0, D)

        def small_in():
            nc.vector.tensor_copy(out=bc_f[:], in_=bc_bf[:])
            nc.vector.tensor_copy(out=alpha[:], in_=alpha_bf[:])
            nc.vector.tensor_copy(out=beta[:], in_=beta_bf[:])

        def centres_add(b, h):
            rows = slice(G * b + 2 * h, G * b + 2 * h + 2)
            nc.vector.tensor_tensor(
                out=x_rows[:, rows, :], in0=cl_sb[:, rows, :], in1=bias_sb[:, 2 * h : 2 * h + 2, :], op=ALU.add
            )

        def centres_turn(b, h):
            live["x", b, h] = words_onto_partitions(x_rows, G * b + 2 * h)

        def centres_regroup(b, h, copy):
            regroup(x_grouped, M * b + PAIR * h, ("x", b, h), copy)

        def centres_in_quantise(b):
            quantise(x_grouped, x_codes, x_scales, M * b, M)

        def centres_matmul(b):
            for t in range(G):
                z = bank("z")
                nc.tensor.matmul_mx(
                    out=z[:],
                    lhsT=w_codes[:, P * t : P * t + P].bitcast(FP8X4),
                    lhsT_scale=w_scales[:, P * t : P * t + P],
                    rhs=x_codes[:, M * b : M * b + M].bitcast(FP8X4),
                    rhs_scale=x_scales[:, M * b : M * b + M],
                    start=True,
                    stop=True,
                )
                nc.scalar.activation(
                    out=c_sb[b][:, t, :], in_=z[:], func=ACT.Silu, bias=bc_f[:, t : t + 1], scale=1.0
                )

        def centres_turn_back(b, g):
            first = P * g
            ct = bank("ct")
            for t in range(G):
                nc.tensor.transpose(ct[:, P * t : P * t + P], c_sb[b][:, t, first : first + P], identity[:])
            live["ct", b, g] = ct

        def centres_squares(b, g):
            col = G * b + g
            nc.scalar.activation(
                out=squares[:], in_=live["ct", b, g][:], func=ACT.Square, accum_out=c_sumsq[:, col : col + 1]
            )

        def centres_norm(b, first, groups):
            reciprocal_norm(c_rnorm, c_clamped, c_sumsq, G * b + first, groups)

        def centres_spread(b, h):
            rn = factor_bank("rn_c", PAIR)
            for side in range(2):
                col = G * b + 2 * h + side
                spread(rn[:, P * side : P * side + P], c_rnorm[:, col : col + 1])
            live["rn_c", b, h] = rn

        def centres_scale(b, h):
            cols = slice(M * b + PAIR * h, M * b + PAIR * h + PAIR)
            nc.vector.tensor_tensor(
                out=c_grouped[:, cols, :].rearrange("p (c i) t -> p c t i", i=RUN),
                in0=live["rn_c", b, h][:]
                .rearrange("p (c i) -> p c i", i=RUN)
                .unsqueeze(2)
                .to_broadcast([P, PAIR // RUN, G, RUN]),
                in1=c_sb[b][:, :, PAIR * h : PAIR * h + PAIR].rearrange("p t (c i) -> p c t i", i=RUN),
                op=ALU.mult,
            )

        def centres_quantise(b):
            quantise(c_grouped, c_codes, c_scales, M * b, M)

        def block_columns(block):
            chunk, j = divmod(block, 2)
            return chunk, BLOCK * j

        def points_gram(block):
            chunk, first = block_columns(block)
            gram = bank("gram", BLOCK)
            for j in range(2):
                cols = slice(first + P * j, first + P * j + P)
                for t in range(G):
                    nc.tensor.matmul(
                        gram[:, P * j : P * j + P],
                        lhsT=pts[chunk][:, t, cols],
                        rhs=pts[chunk][:, t, cols],
                        start=t == 0,
                        stop=t == G - 1,
                    )
            live["gram", block] = gram

        def points_diagonal(block):
            for j in range(2):
                col = 2 * block + j
                nc.vector.scalar_tensor_tensor(
                    out=diagonal[:],
                    in0=live["gram", block][:, P * j : P * j + P],
                    scalar=1.0,
                    in1=identity[:],
                    op0=ALU.mult,
                    op1=ALU.mult,
                    accum_out=p_sumsq[:, col : col + 1],
                )

        def points_turn(block):
            chunk, first = block_columns(block)
            f = bank("f")
            words = pts[chunk][:].bitcast(F32)
            for t in range(G):
                nc.tensor.transpose(
                    f[:, P * t : P * t + P], words[:, t, first // 2 : first // 2 + P], identity[:]
                )
            live["f", block] = f

        def points_squares(block):
            pairs = live["f", block][:].bitcast(BF16).rearrange("w (d e) -> w e d", e=2)
            for e in range(2):
                col = 2 * block + e
                nc.scalar.activation(
                    out=squares[:], in_=pairs[:, e, :], func=ACT.Square, accum_out=p_sumsq[:, col : col + 1]
                )

        def points_square(block):
            chunk, first = block_columns(block)
            src = pts[chunk][:, :, first : first + BLOCK]
            sq = work.tile([P, G, BLOCK], F32, name="sq", tag="sq", bufs=2)
            nc.gpsimd.tensor_tensor(out=sq[:], in0=src, in1=src, op=ALU.mult)
            live["sq", block] = sq

        def points_sums(block):
            sums = bank("sums", 2)
            for j in range(2):
                for t in range(G):
                    nc.tensor.matmul(
                        sums[:, j : j + 1],
                        lhsT=live["sq", block][:, t, P * j : P * j + P],
                        rhs=ones[:],
                        start=t == 0,
                        stop=t == G - 1,
                    )
            live["sums", block] = sums

        def points_sums_norm(block):
            clamped = work.tile([P, 2], F32, name="clamped", tag="clamped", bufs=2)
            nc.vector.tensor_scalar(
                out=clamped[:], in0=live["sums", block][:], scalar1=NORM_EPS_SQUARED, scalar2=None, op0=ALU.max
            )
            nc.gpsimd.tensor_tensor(
                out=p_rnorm[:, 2 * block : 2 * block + 2], in0=clamped[:], in1=minus_half[:, 0:2], op=ALU.pow
            )

        def points_norm(block, blocks):
            reciprocal_norm(p_rnorm, p_clamped, p_sumsq, 2 * block, 2 * blocks)

        def points_spread(block):
            rn = factor_bank("rn_p", BLOCK)
            for e in range(2):
                spread(rn[:, P * e : P * e + P], p_rnorm[:, 2 * block + e : 2 * block + e + 1])
            live["rn_p", block] = rn

        def points_spread_copy(block):
            rn = work.tile([P, BLOCK], F32, name="rn_sb", tag="rn_sb", bufs=2)
            nc.scalar.copy(out=rn[:], in_=live["rn_p", block][:])
            live["rn_p", block] = rn

        def points_scale(block, engine, skip=0, width=BLOCK):
            chunk, first = block_columns(block)
            rn = live["rn_p", block]
            dst = p_grouped[:, BLOCK * block + skip : BLOCK * block + skip + width, :]
            src = pts[chunk][:, :, first + skip : first + skip + width]
            if block in GRAM:
                engine.tensor_tensor(
                    out=dst.rearrange("p (c i) t -> p c t i", i=RUN),
                    in0=rn[:, skip : skip + width]
                    .rearrange("p (c i) -> p c i", i=RUN)
                    .unsqueeze(2)
                    .to_broadcast([P, width // RUN, G, RUN]),
                    in1=src.rearrange("p t (c i) -> p c t i", i=RUN),
                    op=ALU.mult,
                )
            else:
                pairs = rn[:].rearrange("p (e w) -> p w e", e=2)[:, skip // 2 : (skip + width) // 2, :]
                engine.tensor_tensor(
                    out=dst.rearrange("p (w e) t -> p w t e", e=2),
                    in0=pairs.unsqueeze(2).to_broadcast([P, width // 2, G, 2]),
                    in1=src.rearrange("p t (w e) -> p w t e", e=2),
                    op=ALU.mult,
                )

        def points_quantise(chunk):
            b, half = divmod(chunk, CHUNKS_PER_BATCH)
            quantise(p_grouped, p_codes, p_scales, N * b + CHUNK * half, CHUNK)

        def similarities(chunk, g):
            b, half = divmod(chunk, CHUNKS_PER_BATCH)
            s = bank("s")
            first = M * b + P * g
            cols = slice(N * b + CHUNK * half, N * b + CHUNK * half + CHUNK)
            nc.tensor.matmul_mx(
                out=s[:],
                lhsT=c_codes[:, first : first + P].bitcast(FP8X4),
                lhsT_scale=c_scales[:, first : first + P],
                rhs=p_codes[:, cols].bitcast(FP8X4),
                rhs_scale=p_scales[:, cols],
                start=True,
                stop=True,
            )
            live["s", chunk, g] = s

        def logits(chunk, g):
            if g == 0:
                live["l", chunk] = work.tile([P, G, CHUNK], F32, name="logit", tag="logit", bufs=2)
            nc.scalar.activation(
                out=live["l", chunk][:, g, :],
                in_=live["s", chunk, g][:],
                func=ACT.Identity,
                bias=beta[:, g : g + 1],
                scale=alpha[:, g : g + 1],
            )

        def first_logits():
            for g in range(G):
                similarities(0, g)
                logits(0, g)

        def points_onto_partitions(k):
            chunk, quarter = divmod(k, TILES_PER_CHUNK)
            lt = bank("lt")
            for g in range(G):
                nc.tensor.transpose(
                    lt[:, P * g : P * g + P], live["l", chunk][:, g, P * quarter : P * quarter + P], identity[:]
                )
            live["lt", k] = lt

        def row_max(k):
            neg_max = work.tile([P, 1], F32, name="neg_max", tag="neg_max", bufs=6)
            nc.vector.tensor_reduce(out=neg_max[:], in_=live["lt", k][:], axis=AX.X, op=ALU.max, negate=True)
            live["max", k] = neg_max

        def exponentials(k):
            ex = work.tile([P, M], F32, name="ex", tag="ex", bufs=8)
            total = work.tile([P, 1], F32, name="total", tag="total", bufs=6)
            nc.scalar.activation(
                out=ex[:], in_=live["lt", k][:], func=ACT.Exp, bias=live["max", k][:], scale=1.0, accum_out=total[:]
            )
            live["ex", k] = ex
            live["total", k] = total

        def normalise(k):
            share = work.tile([P, 1], F32, name="share", tag="share", bufs=6)
            nc.vector.reciprocal(out=share[:], in_=live["total", k][:])
            ex = live["ex", k]
            if k < TILES - 2:
                nc.gpsimd.tensor_scalar(
                    out=ex[:], in0=ex[:], scalar1=share[:], scalar2=0.0, op0=ALU.mult, op1=ALU.add
                )
            else:
                nc.vector.tensor_scalar(out=ex[:], in0=ex[:], scalar1=share[:], scalar2=None, op0=ALU.mult)

        def clusters_onto_partitions(k):
            o = bank("o")
            for g in range(G):
                nc.tensor.transpose(o[:, P * g : P * g + P], live["ex", k][:, P * g : P * g + P], identity[:])
            live["o", k] = o

        def copy_out(k):
            together = 2 if k < TILES - 2 else 1
            place = k % together
            if place == 0:
                live["out"] = work.tile([P, G, P * together], F32, name="result", tag="result" + str(together), bufs=7)
            result = live["out"]
            copy = nc.scalar.copy if k in SCALAR_COPIES else nc.vector.tensor_copy
            copy(
                out=result[:, :, P * place : P * place + P],
                in_=live["o", k][:].rearrange("p (g n) -> p g n", g=G),
            )
            if place == together - 1:
                b, quarter = divmod(k + 1 - together, N // P)
                first = P * quarter
                nc.sync.dma_start(
                    out=out[b].rearrange("(p g) n -> p g n", g=G)[:, :, first : first + P * together], in_=result[:]
                )

        def softmax_step(step):
            if 0 <= step + 1 < TILES:
                points_onto_partitions(step + 1)
            if 0 <= step < TILES:
                row_max(step)
            if 0 <= step - 6 < TILES:
                copy_out(step - 6)
            if 0 <= step - 2 < TILES:
                normalise(step - 2)
            for chunk, g in SIMILARITIES_IN.get(step, ()):
                similarities(chunk, g)
            for chunk, g in LOGITS_IN.get(step, ()):
                logits(chunk, g)
            if 0 <= step < TILES:
                exponentials(step)
            if 0 <= step - 4 < TILES:
                clusters_onto_partitions(step - 4)

        sc, vc = nc.scalar.copy, nc.vector.tensor_copy
        ve, ge = nc.vector, nc.gpsimd
        weights_turn(0)
        weights_turn(1)
        weights_regroup(0, sc)
        weights_regroup(1, sc)
        small_in()
        centres_add(0, 0)
        centres_turn(0, 0)
        centres_regroup(0, 0, sc)
        centres_add(0, 1)
        centres_turn(0, 1)
        weights_quantise()
        centres_regroup(0, 1, sc)
        points_turn(0)
        points_squares(0)
        points_norm(0, 1)
        centres_in_quantise(0)
        points_gram(1)
        centres_matmul(0)
        centres_add(1, 0)
        centres_add(1, 1)
        points_diagonal(1)
        points_norm(1, 1)
        points_square(6)
        points_spread(0)
        centres_turn(1, 0)
        centres_turn(1, 1)
        points_scale(0, ve)
        centres_regroup(1, 0, sc)
        centres_regroup(1, 1, vc)
        centres_turn_back(0, 0)
        centres_turn_back(0, 1)
        centres_squares(0, 0)
        centres_squares(0, 1)
        centres_norm(0, 0, 2)
        centres_in_quantise(1)
        points_spread(1)
        points_scale(1, ve)
        centres_turn_back(0, 2)
        centres_turn_back(0, 3)
        centres_squares(0, 2)
        centres_squares(0, 3)
        centres_norm(0, 2, 2)
        points_gram(2)
        points_diagonal(2)
        centres_matmul(1)
        points_gram(3)
        points_diagonal(3)
        points_norm(2, 2)
        points_quantise(0)
        centres_spread(0, 0)
        centres_scale(0, 0)
        points_turn(5)
        points_squares(5)
        centres_spread(0, 1)
        centres_scale(0, 1)
        centres_turn_back(1, 0)
        centres_turn_back(1, 1)
        centres_squares(1, 0)
        centres_squares(1, 1)
        centres_norm(1, 0, 2)
        points_gram(4)
        points_diagonal(4)
        points_norm(4, 2)
        points_spread(2)
        points_spread(3)
        centres_quantise(0)
        points_scale(2, ve)
        points_sums(6)
        points_sums_norm(6)
        exponential_table()
        for g in range(G):
            similarities(0, g)
        for g in range(G):
            logits(0, g)
        centres_spread(1, 0)
        points_scale(3, ve)
        points_quantise(1)
        centres_scale(1, 0)
        centres_turn_back(1, 2)
        centres_turn_back(1, 3)
        centres_squares(1, 2)
        centres_squares(1, 3)
        centres_norm(1, 2, 2)
        points_turn(7)
        points_spread(5)
        points_spread_copy(5)
        points_scale(5, ge)
        between = {
            -1: lambda: (points_squares(7), points_norm(7, 1),),
            0: lambda: (points_spread(4), points_scale(4, ve),),
            1: lambda: (centres_spread(1, 1), centres_scale(1, 1),),
            2: lambda: (points_quantise(2), centres_quantise(1),),
            3: lambda: (points_spread(6), points_scale(6, ve), points_spread(7),),
            4: lambda: (points_scale(7, ve),),
            5: lambda: (points_quantise(3),),
        }
        for step in range(-2, TILES + 6):
            softmax_step(step)
            if step in between:
                between[step]()
